import numpy as np
import ml_dtypes


def mxq(x, axis, fmt="e4m3"):
    dtype, down = {"e4m3": (ml_dtypes.float8_e4m3fn, 7), "e5m2": (ml_dtypes.float8_e5m2, 14)}[fmt]
    v = np.moveaxis(np.asarray(x, np.float32).astype(ml_dtypes.bfloat16).astype(np.float64), axis, -1)
    blocks = v.reshape(v.shape[:-1] + (-1, 32))
    amax = np.abs(blocks).max(-1, keepdims=True)
    byte = np.maximum(np.where(amax > 0, np.frexp(amax)[1] - 1 + 127, 0) - down, 1)
    scale = np.exp2(byte - 127.0)
    codes = (blocks / scale).astype(np.float32).astype(dtype).astype(np.float64)
    return np.moveaxis((codes * scale).reshape(v.shape), -1, axis)


WIDE = False


def mx_kscale(k):
    if not WIDE:
        return np.ones(k)
    levels = np.array([10, -10, 5, -5, 0])
    if k % 512:
        return np.exp2(np.random.permutation(np.resize(levels, k // 32))).repeat(32)
    a = np.empty((k // 512, 16))
    for p in range(k // 512):
        a[p, :8] = np.random.permutation(np.resize(levels, 8))
        for g in range(8):
            far = levels[np.abs(levels - a[p, g]) >= 10]
            a[p, g + 8] = far[np.random.randint(len(far))]
    return np.exp2(a.ravel()).repeat(32)


BF16 = ml_dtypes.bfloat16


def bf(x):
    return np.asarray(x, np.float32).astype(BF16)


def f64(x):
    return np.asarray(x).astype(np.float64)


B, K, DIM = 5120, 1024, 512


def setup_inputs():
    t = mx_kscale(DIM)
    t = t / t.min()
    x = np.random.standard_normal((B, DIM)) * 1.2 / DIM ** 0.25
    centers = np.random.uniform(size=(K, DIM)) * 1.6 / DIM ** 0.25
    D = 0.6 * np.random.uniform(size=(K, DIM)) + 0.7
    sign = np.where(np.random.uniform(size=(K, DIM)) < 0.25, -1.0, 1.0)
    return {"x": bf(x * t), "centers": bf(centers * t), "D": bf(D * sign * t * t)}


def reference(x, centers, D):
    x, centers, D = f64(x), f64(centers), f64(D)
    D_abs = np.abs(D) + 1e-4
    D_inv = 1.0 / D_abs
    log_det = np.sum(np.log(D_abs), axis=1)
    det_scale_factor = -0.5 * log_det
    det_scale_safe = np.exp(det_scale_factor - np.max(det_scale_factor))
    x2 = mxq(x * x, 1, "e4m3") @ mxq(D_inv, 1, "e4m3").T
    xc = mxq(x, 1, "e4m3") @ mxq(centers * D_inv, 1, "e4m3").T
    c2 = np.sum(centers * centers * D_inv, axis=1)
    dist_sq = x2 - 2.0 * xc + c2[None, :]
    expo = -0.5 * dist_sq
    expo_safe = expo - np.max(expo, axis=-1, keepdims=True)
    numer_safe = det_scale_safe[None, :] * np.exp(expo_safe)
    denom_safe = np.sum(numer_safe, axis=1, keepdims=True)
    resp = numer_safe / denom_safe
    return resp

@@ -1,0 +1,601 @@
+from contextlib import ExitStack
+
+import concourse.mybir as mybir
+from concourse.masks import make_identity
+
+F32 = mybir.dt.float32
+BF16 = mybir.dt.bfloat16
+I32 = mybir.dt.int32
+U32 = mybir.dt.uint32
+U8 = mybir.dt.uint8
+FP8X4 = mybir.dt.float8_e4m3fn_x4
+ALU = mybir.AluOpType
+ACT = mybir.ActivationFunctionType
+AX = mybir.AxisListType
+
+P = 128
+ROWS = 5120
+CLS = 1024
+DIM = 512
+NT = ROWS // P
+NB = NT // 4
+CT = CLS // P
+HC = CLS // 2
+EPS = 1e-4
+
+FLOPS = 2 * 2 * ROWS * CLS * DIM
+PIN = True
+XG_BUFS = 4
+XQ_BUFS = 7
+O4_BUFS = 4
+ST_BUFS = 3
+PRE = 4
+OFF = {"xtr":-16,"xcp":-15,"xq0":-12,"xsq":-13,"xq1":-9,"mt":-6,"md":-6,"ev":-5,"ad":-5,"bt":-1,"em":0,"ex":0,"rc":1,"sc":4}
+SQE = "VG"
+N_LO = -16
+N_HI = 4
+PRE_Q1 = 2
+LASTV = 1
+SQM = ["","","","","SG","VG","SG","VG","SG","VG"]
+LAST1 = 2
+
+
+def tile_axis_aligned_gmm_layer_t_kernel(tc, x, centers, D, out):
+    nc = tc.nc
+    with ExitStack() as ctx:
+        if PIN:
+            ctx.enter_context(tc.manual_schedule())
+        const = ctx.enter_context(tc.tile_pool(name="const", bufs=1))
+        small = ctx.enter_context(tc.tile_pool(name="small", bufs=6))
+        xgp = ctx.enter_context(tc.tile_pool(name="xgp", bufs=XG_BUFS))
+        xqp = ctx.enter_context(tc.tile_pool(name="xqp", bufs=XQ_BUFS))
+        ps = ctx.enter_context(tc.psum_pool(name="ps", bufs=2))
+
+        def bank(nm, tag):
+            return ps.tile([P, 512], F32, name=nm, tag=tag)
+
+        one = const.tile([P, 1], F32, name="one", tag="one")
+        nc.vector.memset(one[:], 1.0)
+        warm = const.tile([P, 1], F32, name="warm", tag="warm")
+        nc.scalar.activation(out=warm[:], in_=one[:], func=ACT.Ln)
+        ident = const.tile([P, P], F32, name="ident", tag="ident")
+        make_identity(nc, ident[:])
+        half_c = const.tile([P, P], F32, name="half_c", tag="half_c")
+        nc.vector.memset(half_c[:], 0.5)
+
+        x_sb = const.tile([P, NT * DIM], BF16, name="x_sb", tag="x_sb")
+        w1c = const.tile([P, CLS], U32, name="w1c", tag="w1c", align_bytes=64)
+        w2c = const.tile([P, CLS], U32, name="w2c", tag="w2c", align_bytes=64)
+        w1s = const.tile([P, CLS], U8, name="w1s", tag="w1s", align_bytes=64)
+        w2s = const.tile([P, CLS], U8, name="w2s", tag="w2s", align_bytes=64)
+        g_b = const.tile([P, CLS], F32, name="g_b", tag="g_b")
+        gcol = const.tile([P, 4], F32, name="gcol", tag="gcol")
+        a0 = const.tile([P, 1], F32, name="a0", tag="a0")
+        inv = const.tile([P, 1], F32, name="inv", tag="inv")
+        einv = const.tile([P, 1], F32, name="einv", tag="einv")
+        lninv = const.tile([P, 1], F32, name="lninv", tag="lninv")
+        x_w = x_sb[:].bitcast(F32)
+        x_v = x.rearrange("(p t) d -> p t d", t=NT)
+        out_v = out.rearrange("(p t) k -> p t k", t=NT)
+        d_v = D.rearrange("(j p) d -> p j d", p=P)
+        c_v = centers.rearrange("(j p) d -> p j d", p=P)
+
+        xg = {}
+        xt = {}
+        xq = {}
+        xs = {}
+
+        def x_tr(b, half):
+            if half == 0:
+                xg[b] = xgp.tile([P, 2 * 2048], BF16, name="xg", tag="xg", align_bytes=64)
+                xq[b] = xqp.tile([P, 1024], U32, name="xq", tag="xq", align_bytes=64)
+                xs[b] = xqp.tile([P, 1024], U8, name="xs", tag="xs", align_bytes=64)
+            xt[(b, half)] = bank("xT", "pd")
+            for i in range(2):
+                t = 4 * b + 2 * half + i
+                for u in range(2):
+                    dst = (2 * i + u) * P
+                    src = t * 256
+                    nc.tensor.transpose(
+                        out=xt[(b, half)][:, dst : dst + P], in_=x_w[:, src + u : src + 256 : 2], identity=ident[:]
+                    )
+
+        def x_cp(b, half, eng):
+            o_ap = xg[b][:].bitcast(F32)[:, half * 512 : (half + 1) * 512].rearrange("p (i r u) -> p i r u", i=2, u=2)
+            i_ap = xt[(b, half)][:].rearrange("p (i u r) -> p i r u", i=2, u=2)
+            if eng == "V":
+                nc.vector.tensor_copy(out=o_ap, in_=i_ap)
+            else:
+                nc.scalar.copy(out=o_ap, in_=i_ap)
+
+        def x_sq(b, z, eng):
+            zi = slice(z * 1024, (z + 1) * 1024)
+            zo = slice(2048 + z * 1024, 2048 + (z + 1) * 1024)
+            if eng == "S":
+                nc.scalar.activation(out=xg[b][:, zo], in_=xg[b][:, zi], func=ACT.Square)
+            elif eng == "V":
+                nc.vector.tensor_tensor(out=xg[b][:, zo], in0=xg[b][:, zi], in1=xg[b][:, zi], op=ALU.mult)
+            else:
+                nc.gpsimd.tensor_tensor(out=xg[b][:, zo], in0=xg[b][:, zi], in1=xg[b][:, zi], op=ALU.mult)
+
+        def x_qt(b, kind):
+            nc.vector.quantize_mx(
+                out=xq[b][:, kind * 512 : (kind + 1) * 512].bitcast(FP8X4),
+                scales=xs[b][:, kind * 512 : (kind + 1) * 512],
+                in_=xg[b][:, kind * 2048 : (kind + 1) * 2048],
+            )
+
+        with tc.tile_pool(name="pro", bufs=1) as pro:
+            d_sb = pro.tile([P, CT * DIM], BF16, name="d_sb", tag="d_sb")
+            c_sb = pro.tile([P, CT * DIM], BF16, name="c_sb", tag="c_sb")
+            for src_v, dst_t in ((d_v, d_sb), (c_v, c_sb)):
+                for h in range(2):
+                    cols = slice(h * 4 * DIM, (h + 1) * 4 * DIM)
+                    nc.sync.dma_start(
+                        out=dst_t[:, cols].rearrange("p (j d) -> p j d", j=4), in_=src_v[:, 4 * h : 4 * h + 4, :]
+                    )
+            for c in range(5):
+                nc.sync.dma_start(
+                    out=x_sb[:, c * 8 * DIM : (c + 1) * 8 * DIM].rearrange("p (t d) -> p t d", t=8),
+                    in_=x_v[:, 8 * c : 8 * c + 8, :],
+                )
+            d_i = d_sb[:].bitcast(I32)
+            d_w = d_sb[:].bitcast(F32)
+            c_w = c_sb[:].bitcast(F32)
+            cg = pro.tile([P, CLS * 4], BF16, name="cg", tag="cg")
+            cg_w = cg[:].bitcast(F32)
+            w1g = pro.tile([P, CLS * 4], BF16, name="w1g", tag="w1g", align_bytes=64)
+            w2g = pro.tile([P, CLS * 4], BF16, name="w2g", tag="w2g", align_bytes=64)
+            lnr = [pro.tile([P, 4 * HC], F32, name="lnr%d" % h, tag="lnr%d" % h) for h in range(2)]
+            dv = [pro.tile([P, 4 * HC], F32, name="dv%d" % h, tag="dv%d" % h) for h in range(2)]
+            csq = [pro.tile([P, 4 * HC], F32, name="csq%d" % h, tag="csq%d" % h) for h in range(2)]
+            d_t = {}
+            c_t = {}
+            g_p = {}
+
+            def p_and(h):
+                words = slice(h * 1024, (h + 1) * 1024)
+                nc.vector.tensor_single_scalar(
+                    out=d_i[:, words], in_=d_i[:, words], scalar=0x7FFF7FFF, op=ALU.bitwise_and
+                )
+
+            def p_dtr(h):
+                for u in range(2):
+                    d_t[(h, u)] = bank("dT", "pa" if h == 0 else "pb")
+                    for jj in range(4):
+                        src = (4 * h + jj) * 256
+                        nc.tensor.transpose(
+                            out=d_t[(h, u)][:, jj * P : (jj + 1) * P], in_=d_w[:, src + u : src + 256 : 2], identity=ident[:]
+                        )
+
+            def p_rho():
+                nc.vector.tensor_scalar_add(out=a0[:], in0=d_t[(0, 0)][:].bitcast(BF16)[:, 0:1], scalar1=EPS)
+                nc.vector.reciprocal(out=inv[:], in_=a0[:])
+                nc.vector.tensor_scalar_mul(out=einv[:], in0=inv[:], scalar1=EPS)
+                nc.scalar.activation(out=lninv[:], in_=inv[:], func=ACT.Ln)
+
+            def p_ln(h, u):
+                nc.scalar.activation(
+                    out=lnr[h][:, 2 * u * HC : (2 * u + 2) * HC].rearrange("p (e r) -> p e r", e=2),
+                    in_=d_t[(h, u)][:].bitcast(BF16).rearrange("p (r e) -> p e r", e=2),
+                    func=ACT.Ln,
+                    scale=inv[:, 0:1],
+                    bias=einv[:, 0:1],
+                )
+
+            def p_ctr(h, pr):
+                c_t[(h, pr)] = bank("cT", "pc" if h == 0 else "pd")
+                for jj in range(2):
+                    for u in range(2):
+                        src = (4 * h + 2 * pr + jj) * 256
+                        dst = (2 * jj + u) * P
+                        nc.tensor.transpose(
+                            out=c_t[(h, pr)][:, dst : dst + P], in_=c_w[:, src + u : src + 256 : 2], identity=ident[:]
+                        )
+
+            def p_cgc(h, pr):
+                w0 = (4 * h + 2 * pr) * P * 2
+                nc.vector.tensor_copy(
+                    out=cg_w[:, w0 : w0 + 512].rearrange("p (j r u) -> p j r u", j=2, u=2),
+                    in_=c_t[(h, pr)][:].rearrange("p (j u r) -> p j r u", j=2, u=2),
+                )
+
+            def p_csq(h, eng):
+                cg_t = cg[:, h * 4 * HC : (h + 1) * 4 * HC].rearrange("p (r t) -> p t r", t=4)
+                cs_t = csq[h][:].rearrange("p (t r) -> p t r", t=4)
+                if eng == "V":
+                    nc.vector.tensor_tensor(out=cs_t, in0=cg_t, in1=cg_t, op=ALU.mult)
+                elif eng == "S":
+                    nc.scalar.activation(out=cs_t, in_=cg_t, func=ACT.Square)
+                else:
+                    nc.gpsimd.tensor_tensor(out=cs_t, in0=cg_t, in1=cg_t, op=ALU.mult)
+
+            def p_gl(h, t):
+                if t == 0:
+                    g_p[h] = bank("gP", "pa")
+                nc.tensor.matmul(
+                    out=g_p[h][:], lhsT=half_c[:], rhs=lnr[h][:, t * HC : (t + 1) * HC], start=(t == 0), stop=False
+                )
+
+            def p_exp(h, pc):
+                rr = slice(pc * 256, (pc + 1) * 256)
+                nc.scalar.activation(
+                    out=dv[h][:].rearrange("p (t r) -> p t r", t=4)[:, :, rr],
+                    in_=lnr[h][:].rearrange("p (t r) -> p t r", t=4)[:, :, rr],
+                    func=ACT.Exp,
+                    scale=-1.0,
+                    bias=lninv[:, 0:1],
+                )
+
+            def p_w1(h, pc, eng):
+                rr = slice(pc * 256, (pc + 1) * 256)
+                gcols = slice((h * HC + pc * 256) * 4, (h * HC + (pc + 1) * 256) * 4)
+                if eng == "S":
+                    nc.scalar.activation(
+                        out=w1g[:, gcols].rearrange("p (r t) -> p r t", t=4),
+                        in_=dv[h][:].rearrange("p (t r) -> p r t", t=4)[:, rr, :],
+                        func=ACT.Copy,
+                        scale=0.5,
+                    )
+                    return
+                e = nc.gpsimd if eng == "G" else nc.vector
+                e.tensor_scalar(
+                    out=w1g[:, gcols].rearrange("p (r t) -> p r t", t=4),
+                    in0=dv[h][:].rearrange("p (t r) -> p r t", t=4)[:, rr, :],
+                    scalar1=0.5,
+                    scalar2=0.0,
+                    op0=ALU.mult,
+                    op1=ALU.add,
+                )
+
+            def p_w2(h, pc):
+                rr = slice(pc * 256, (pc + 1) * 256)
+                gcols = slice((h * HC + pc * 256) * 4, (h * HC + (pc + 1) * 256) * 4)
+                nc.vector.scalar_tensor_tensor(
+                    out=w2g[:, gcols].rearrange("p (r t) -> p r t", t=4),
+                    in0=dv[h][:].rearrange("p (t r) -> p r t", t=4)[:, rr, :],
+                    scalar=-1.0,
+                    in1=cg[:, gcols].rearrange("p (r t) -> p r t", t=4),
+                    op0=ALU.mult,
+                    op1=ALU.mult,
+                )
+
+            def p_qw(h, which):
+                hc = slice(h * HC, (h + 1) * HC)
+                hg = slice(h * HC * 4, (h + 1) * HC * 4)
+                if which == 1:
+                    nc.vector.quantize_mx(out=w1c[:, hc].bitcast(FP8X4), scales=w1s[:, hc], in_=w1g[:, hg])
+                else:
+                    nc.vector.quantize_mx(out=w2c[:, hc].bitcast(FP8X4), scales=w2s[:, hc], in_=w2g[:, hg])
+
+            def p_q(h, t, eng):
+                ts = slice(t * HC, (t + 1) * HC)
+                e = nc.gpsimd if eng == "G" else nc.vector
+                e.tensor_tensor(out=csq[h][:, ts], in0=dv[h][:, ts], in1=csq[h][:, ts], op=ALU.mult)
+
+            def p_gq(h, t):
+                ts = slice(t * HC, (t + 1) * HC)
+                nc.tensor.matmul(out=g_p[h][:], lhsT=half_c[:], rhs=csq[h][:, ts], start=False, stop=(t == 3))
+
+            def p_gb(h):
+                nc.scalar.copy(out=g_b[:, h * HC : (h + 1) * HC], in_=g_p[h][:])
+
+            def p_gcol():
+                g_t = bank("gT", "pb")
+                for jj in range(4):
+                    nc.tensor.transpose(
+                        out=g_t[:, jj * P : (jj + 1) * P], in_=g_b[:, jj * P : (jj + 1) * P], identity=ident[:]
+                    )
+                nc.vector.tensor_copy(
+                    out=gcol[:].rearrange("p (j o) -> p j o", o=1),
+                    in_=g_t[:].rearrange("p (j r) -> p j r", j=4)[:, :, 0:1],
+                )
+
+            glcol = pro.tile([P, 4], F32, name="glcol", tag="glcol")
+            gl_b = pro.tile([P, HC], F32, name="gl_b", tag="gl_b")
+            c2col = [pro.tile([P, 4], F32, name="c2col%d" % h, tag="c2col%d" % h) for h in range(2)]
+            c2h = pro.tile([P, 4], F32, name="c2h", tag="c2h")
+            q_a = {}
+
+            def p_gl2(h, t):
+                if t == 0:
+                    g_p[h] = bank("gP", "pa")
+                nc.tensor.matmul(
+                    out=g_p[h][:], lhsT=half_c[:], rhs=lnr[h][:, t * HC : (t + 1) * HC], start=(t == 0), stop=(t == 3)
+                )
+
+            def p_glc():
+                nc.scalar.copy(out=g_b[:, 0:HC], in_=g_p[0][:])
+                g_t = bank("gT", "pa")
+                for jj in range(4):
+                    nc.tensor.transpose(
+                        out=g_t[:, jj * P : (jj + 1) * P], in_=g_b[:, jj * P : (jj + 1) * P], identity=ident[:]
+                    )
+                nc.scalar.copy(
+                    out=glcol[:].rearrange("p (j o) -> p j o", o=1),
+                    in_=g_t[:].rearrange("p (j r) -> p j r", j=4)[:, :, 0:1],
+                )
+
+            def p_glb():
+                nc.scalar.copy(out=gl_b[:], in_=g_p[1][:])
+
+            def p_qp(h, pc, eng):
+                rr = slice(pc * 256, (pc + 1) * 256)
+                e = nc.gpsimd if eng == "G" else nc.vector
+                e.tensor_tensor(
+                    out=csq[h][:].rearrange("p (t r) -> p t r", t=4)[:, :, rr],
+                    in0=dv[h][:].rearrange("p (t r) -> p t r", t=4)[:, :, rr],
+                    in1=csq[h][:].rearrange("p (t r) -> p t r", t=4)[:, :, rr],
+                    op=ALU.mult,
+                )
+
+            def p_at(h, jj, tag):
+                if jj == 0:
+                    q_a[h] = bank("qA", tag)
+                for t in range(4):
+                    nc.tensor.matmul(
+                        out=q_a[h][:, jj * P : (jj + 1) * P],
+                        lhsT=csq[h][:, t * HC + jj * P : t * HC + (jj + 1) * P],
+                        rhs=ident[:],
+                        is_transpose=True,
+                        start=(t == 0),
+                        stop=(t == 3),
+                    )
+
+            def p_c2(h):
+                nc.vector.tensor_reduce(
+                    out=c2col[h][:], in_=q_a[h][:].rearrange("p (j r) -> p j r", j=4), axis=AX.X, op=ALU.add
+                )
+                if h == 0:
+                    nc.vector.scalar_tensor_tensor(
+                        out=gcol[:], in0=c2col[0][:], scalar=0.5, in1=glcol[:], op0=ALU.mult, op1=ALU.add
+                    )
+                else:
+                    nc.vector.tensor_scalar_mul(out=c2h[:], in0=c2col[1][:], scalar1=0.5)
+
+            def p_gb2(tag):
+                b_b = bank("bB", tag)
+                for jj in range(4):
+                    nc.tensor.transpose(
+                        out=b_b[:, jj * P : (jj + 1) * P], in_=c2h[:, jj : jj + 1].to_broadcast([P, P]), identity=ident[:]
+                    )
+                nc.vector.tensor_tensor(out=g_b[:, HC:CLS], in0=b_b[:], in1=gl_b[:], op=ALU.add)
+
+            p_and(0)
+            p_and(1)
+            p_dtr(0)
+            p_rho()
+            p_dtr(1)
+            for h in range(2):
+                for u in range(2):
+                    p_ln(h, u)
+            for h in range(2):
+                for pr in range(2):
+                    p_ctr(h, pr)
+                    p_cgc(h, pr)
+            p_csq(0, "V")
+            for t in range(4):
+                p_gl2(0, t)
+            x_tr(0, 0)
+            x_tr(0, 1)
+            p_csq(1, "V")
+            for t in range(4):
+                p_gl2(1, t)
+            for h in range(2):
+                for pc in range(2):
+                    p_exp(h, pc)
+                    p_w1(h, pc, "G")
+                    p_w2(h, pc)
+                p_qw(h, 2)
+                if h == 0:
+                    p_qp(0, 0, "V")
+                    p_qp(0, 1, "V")
+            p_glc()
+            p_glb()
+            for jj in range(4):
+                p_at(0, jj, "pc")
+            p_qp(1, 0, "V")
+            p_qp(1, 1, "V")
+            x_cp(0, 0, "S")
+            x_cp(0, 1, "S")
+            x_tr(1, 0)
+            x_tr(1, 1)
+            p_c2(0)
+            x_sq(0, 0, "S")
+            x_sq(0, 1, "S")
+            x_cp(1, 0, "S")
+            x_cp(1, 1, "S")
+            for jj in range(4):
+                p_at(1, jj, "pc")
+            x_qt(0, 0)
+            p_c2(1)
+            p_gb2("pc")
+            p_qw(0, 1)
+            p_qw(1, 1)
+            x_tr(2, 0)
+            x_tr(2, 1)
+            x_sq(1, 0, "S")
+            x_sq(1, 1, "S")
+            x_cp(2, 0, "S")
+            x_cp(2, 1, "S")
+            x_tr(3, 0)
+            x_tr(3, 1)
+            x_cp(3, 0, "S")
+            x_cp(3, 1, "S")
+            x_sq(2, 0, "G")
+            x_sq(2, 1, "G")
+            x_sq(3, 0, "G")
+            x_sq(3, 1, "G")
+            x_qt(0, 1)
+            x_qt(1, 0)
+            x_qt(1, 1)
+            x_qt(2, 0)
+            x_qt(3, 0)
+
+        work = ctx.enter_context(tc.tile_pool(name="work", bufs=O4_BUFS))
+        stp = ctx.enter_context(tc.tile_pool(name="stp", bufs=ST_BUFS))
+        o4 = {}
+        s_t = {}
+        pt = {}
+        acc = {}
+        st = {}
+        dmin = {}
+        nmin = {}
+        sums = {}
+        rec = {}
+
+        def mx_pair(dst, l1, l1s, r1, r1s, l2, l2s, r2, r2s):
+            nc.tensor.matmul_mx(
+                out=dst, lhsT=l1.bitcast(FP8X4), lhsT_scale=l1s, rhs=r1.bitcast(FP8X4), rhs_scale=r1s,
+                start=True, stop=False,
+            )
+            nc.tensor.matmul_mx(
+                out=dst, lhsT=l2.bitcast(FP8X4), lhsT_scale=l2s, rhs=r2.bitcast(FP8X4), rhs_scale=r2s,
+                start=False, stop=True,
+            )
+
+        def m_t(b, jj):
+            if jj == 0:
+                s_t[b] = stp.tile([P, 4 * 512], F32, name="s_t", tag="s_t")
+            jc = slice(jj * P, (jj + 1) * P)
+            pt[(b, jj)] = bank("pt", "pb")
+            mx_pair(
+                pt[(b, jj)][:], w1c[:, jc], w1s[:, jc], xq[b][:, 512:1024], xs[b][:, 512:1024],
+                w2c[:, jc], w2s[:, jc], xq[b][:, 0:512], xs[b][:, 0:512],
+            )
+
+        def e_v(b, jj, eng):
+            if eng == "S":
+                nc.scalar.activation(
+                    out=s_t[b][:, jj * 512 : (jj + 1) * 512], in_=pt[(b, jj)][:], func=ACT.Identity,
+                    bias=gcol[:, jj : jj + 1], scale=1.0,
+                )
+            else:
+                nc.vector.tensor_scalar_add(
+                    out=s_t[b][:, jj * 512 : (jj + 1) * 512], in0=pt[(b, jj)][:], scalar1=gcol[:, jj : jj + 1]
+                )
+
+        def m_d(b, i):
+            if i == 0:
+                o4[b] = work.tile([P, 4 * CLS], F32, name="o4", tag="o4")
+            rc = slice(i * P, (i + 1) * P)
+            rc2 = slice(512 + i * P, 512 + (i + 1) * P)
+            hc = slice(HC, CLS)
+            acc[(b, i)] = bank("acc", "pc")
+            mx_pair(
+                acc[(b, i)][:], xq[b][:, rc2], xs[b][:, rc2], w1c[:, hc], w1s[:, hc],
+                xq[b][:, rc], xs[b][:, rc], w2c[:, hc], w2s[:, hc],
+            )
+
+        def a_d(b, i):
+            nc.vector.tensor_tensor(
+                out=o4[b][:, i * CLS + HC : (i + 1) * CLS], in0=acc[(b, i)][:], in1=g_b[:, HC:CLS], op=ALU.add
+            )
+
+        def d_m(b):
+            dmin[b] = small.tile([P, 4], F32, name="dmin", tag="dmin")
+            nmin[b] = small.tile([P, 4], F32, name="nmin", tag="nmin")
+            nc.vector.tensor_reduce(
+                out=dmin[b][:], in_=o4[b][:].rearrange("p (i k) -> p i k", i=4)[:, :, HC:CLS], axis=AX.X, op=ALU.min
+            )
+
+        def b_t(b, i):
+            st[(b, i)] = bank("st", "pa")
+            for jj in range(4):
+                nc.tensor.transpose(
+                    out=st[(b, i)][:, jj * P : (jj + 1) * P],
+                    in_=s_t[b][:, jj * 512 + i * P : jj * 512 + (i + 1) * P],
+                    identity=ident[:],
+                )
+
+        def e_m(b, i):
+            nc.vector.tensor_scalar(
+                out=o4[b][:, i * CLS : i * CLS + HC], in0=st[(b, i)][:], scalar1=0.0, scalar2=dmin[b][:, i : i + 1],
+                op0=ALU.add, op1=ALU.min, accum_out=nmin[b][:, i : i + 1],
+            )
+
+        def e_x(b, i):
+            if i == 0:
+                sums[b] = small.tile([P, 4], F32, name="sums", tag="sums")
+                rec[b] = small.tile([P, 4], F32, name="rec", tag="rec")
+            ic = slice(i * CLS, (i + 1) * CLS)
+            nc.scalar.activation(
+                out=o4[b][:, ic], in_=o4[b][:, ic], func=ACT.Exp, bias=nmin[b][:, i : i + 1], scale=-1.0,
+                accum_out=sums[b][:, i : i + 1],
+            )
+
+        def r_c(b):
+            nc.vector.reciprocal(out=rec[b][:], in_=sums[b][:])
+
+        def r_c1(b, i):
+            nc.vector.reciprocal(out=rec[b][:, i : i + 1], in_=sums[b][:, i : i + 1])
+
+        def s_c(b, i, eng="G"):
+            ic = slice(i * CLS, (i + 1) * CLS)
+            if eng == "V":
+                nc.vector.tensor_scalar_mul(
+                    out=o4[b][:, ic], in0=o4[b][:, ic], scalar1=rec[b][:, i : i + 1]
+                )
+            else:
+                nc.gpsimd.tensor_scalar(
+                    out=o4[b][:, ic], in0=o4[b][:, ic], scalar1=rec[b][:, i : i + 1], scalar2=0.0,
+                    op0=ALU.mult, op1=ALU.add,
+                )
+
+        def store1(b, i):
+            nc.sync.dma_start(out=out_v[:, 4 * b + i, :], in_=o4[b][:, i * CLS : (i + 1) * CLS])
+
+        def s_t_ore(b, pr):
+            t0 = 4 * b + 2 * pr
+            nc.sync.dma_start(
+                out=out_v[:, t0 : t0 + 2, :],
+                in_=o4[b][:].rearrange("p (i k) -> p i k", i=4)[:, 2 * pr : 2 * pr + 2, :],
+            )
+
+        def sched(n):
+            todo = {}
+            for key in OFF:
+                m = n - OFF[key]
+                todo[key] = (m // 4, m % 4) if 0 <= m < 4 * NB else None
+            return todo
+
+        for n in range(N_LO, 4 * NB + N_HI + 1):
+            td = sched(n)
+            if td["bt"]:
+                b_t(*td["bt"])
+            if td["xtr"] and td["xtr"][1] % 2 == 0 and td["xtr"][0] >= PRE:
+                x_tr(td["xtr"][0], td["xtr"][1] // 2)
+            if td["mt"]:
+                m_t(*td["mt"])
+            if td["md"]:
+                m_d(*td["md"])
+            if td["em"]:
+                e_m(*td["em"])
+            if td["ev"]:
+                e_v(td["ev"][0], td["ev"][1], "S")
+            if td["ad"]:
+                a_d(*td["ad"])
+                if td["ad"][1] == 3:
+                    d_m(td["ad"][0])
+            if td["ex"]:
+                e_x(*td["ex"])
+            if td["xcp"] and td["xcp"][1] % 2 == 0 and td["xcp"][0] >= PRE:
+                x_cp(td["xcp"][0], td["xcp"][1] // 2, "S")
+            if td["xq0"] and td["xq0"][1] == 0 and td["xq0"][0] >= PRE:
+                x_qt(td["xq0"][0], 0)
+            if td["rc"] and td["rc"][0] >= NB - LASTV:
+                r_c1(*td["rc"])
+                s_c(td["rc"][0], td["rc"][1], "V")
+                store1(*td["rc"])
+            elif td["rc"] and td["rc"][1] == 3:
+                r_c(td["rc"][0])
+            if td["sc"] and td["sc"][0] < NB - LASTV:
+                s_c(*td["sc"])
+                if td["sc"][0] >= NB - LAST1:
+                    store1(*td["sc"])
+                elif td["sc"][1] % 2 == 1:
+                    s_t_ore(td["sc"][0], td["sc"][1] // 2)
+            if td["xsq"] and td["xsq"][1] % 2 == 0 and td["xsq"][0] >= PRE:
+                x_sq(td["xsq"][0], td["xsq"][1] // 2, SQM[td["xsq"][0]][td["xsq"][1] // 2])
+            if td["xq1"] and td["xq1"][1] == 0 and td["xq1"][0] >= PRE_Q1:
+                x_qt(td["xq1"][0], 1)

@@ -24,31 +24,39 @@ HC = CLS // 2
 EPS = 1e-4
 
 FLOPS = 2 * 2 * ROWS * CLS * DIM
-PIN = True
-XG_BUFS = 4
-XQ_BUFS = 7
-O4_BUFS = 4
-ST_BUFS = 3
-PRE = 4
-OFF = {"xtr":-16,"xcp":-15,"xq0":-12,"xsq":-13,"xq1":-9,"mt":-6,"md":-6,"ev":-5,"ad":-5,"bt":-1,"em":0,"ex":0,"rc":1,"sc":4}
-SQE = "VG"
-N_LO = -16
-N_HI = 4
-PRE_Q1 = 2
+
+MT = -6
+EV = -5
+MD = -5
+AD = -4
+BT = -1
+RC = 1
+SC = 3
+XTR = -17
+XCP = -16
+XSQ = -14
+XQ = -9
+X_PRO = 4
+Q_PRO = 3
+M_PRO = 1
+SQE = "SV"
 LASTV = 1
-SQM = ["","","","","SG","VG","SG","VG","SG","VG"]
-LAST1 = 2
+SC_COLS = 512
+O2_BUFS = 9
+XG_BUFS = 4
+ST_BUFS = 4
+FULL = ()
 
 
 def tile_axis_aligned_gmm_layer_t_kernel(tc, x, centers, D, out):
     nc = tc.nc
     with ExitStack() as ctx:
-        if PIN:
-            ctx.enter_context(tc.manual_schedule())
+        ctx.enter_context(tc.manual_schedule())
         const = ctx.enter_context(tc.tile_pool(name="const", bufs=1))
-        small = ctx.enter_context(tc.tile_pool(name="small", bufs=6))
+        small = ctx.enter_context(tc.tile_pool(name="small", bufs=8))
         xgp = ctx.enter_context(tc.tile_pool(name="xgp", bufs=XG_BUFS))
-        xqp = ctx.enter_context(tc.tile_pool(name="xqp", bufs=XQ_BUFS))
+        xqp = ctx.enter_context(tc.tile_pool(name="xqp", bufs=6))
+        stp = ctx.enter_context(tc.tile_pool(name="stp", bufs=ST_BUFS))
         ps = ctx.enter_context(tc.psum_pool(name="ps", bufs=2))
 
         def bank(nm, tag):
@@ -60,16 +68,15 @@ def tile_axis_aligned_gmm_layer_t_kernel(tc, x, centers, D, out):
         nc.scalar.activation(out=warm[:], in_=one[:], func=ACT.Ln)
         ident = const.tile([P, P], F32, name="ident", tag="ident")
         make_identity(nc, ident[:])
-        half_c = const.tile([P, P], F32, name="half_c", tag="half_c")
-        nc.vector.memset(half_c[:], 0.5)
 
         x_sb = const.tile([P, NT * DIM], BF16, name="x_sb", tag="x_sb")
         w1c = const.tile([P, CLS], U32, name="w1c", tag="w1c", align_bytes=64)
         w2c = const.tile([P, CLS], U32, name="w2c", tag="w2c", align_bytes=64)
         w1s = const.tile([P, CLS], U8, name="w1s", tag="w1s", align_bytes=64)
         w2s = const.tile([P, CLS], U8, name="w2s", tag="w2s", align_bytes=64)
-        g_b = const.tile([P, CLS], F32, name="g_b", tag="g_b")
-        gcol = const.tile([P, 4], F32, name="gcol", tag="gcol")
+        g_b = const.tile([P, HC], F32, name="g_b", tag="g_b")
+        gcol = [const.tile([P, 4], F32, name="gcol%d" % h, tag="gcol%d" % h) for h in range(2)]
+        c2col = [const.tile([P, 4], F32, name="c2col%d" % h, tag="c2col%d" % h) for h in range(2)]
         a0 = const.tile([P, 1], F32, name="a0", tag="a0")
         inv = const.tile([P, 1], F32, name="inv", tag="inv")
         einv = const.tile([P, 1], F32, name="einv", tag="einv")
@@ -84,23 +91,24 @@ def tile_axis_aligned_gmm_layer_t_kernel(tc, x, centers, D, out):
         xt = {}
         xq = {}
         xs = {}
+        s_t = {}
+        pt = {}
+        acc = {}
+        st = {}
 
         def x_tr(b, half):
-            if half == 0:
-                xg[b] = xgp.tile([P, 2 * 2048], BF16, name="xg", tag="xg", align_bytes=64)
-                xq[b] = xqp.tile([P, 1024], U32, name="xq", tag="xq", align_bytes=64)
-                xs[b] = xqp.tile([P, 1024], U8, name="xs", tag="xs", align_bytes=64)
             xt[(b, half)] = bank("xT", "pd")
             for i in range(2):
-                t = 4 * b + 2 * half + i
+                src = (4 * b + 2 * half + i) * 256
                 for u in range(2):
                     dst = (2 * i + u) * P
-                    src = t * 256
                     nc.tensor.transpose(
                         out=xt[(b, half)][:, dst : dst + P], in_=x_w[:, src + u : src + 256 : 2], identity=ident[:]
                     )
 
         def x_cp(b, half, eng):
+            if half == 0:
+                xg[b] = xgp.tile([P, 2 * 2048], BF16, name="xg", tag="xg", align_bytes=64)
             o_ap = xg[b][:].bitcast(F32)[:, half * 512 : (half + 1) * 512].rearrange("p (i r u) -> p i r u", i=2, u=2)
             i_ap = xt[(b, half)][:].rearrange("p (i u r) -> p i r u", i=2, u=2)
             if eng == "V":
@@ -108,50 +116,77 @@ def tile_axis_aligned_gmm_layer_t_kernel(tc, x, centers, D, out):
             else:
                 nc.scalar.copy(out=o_ap, in_=i_ap)
 
-        def x_sq(b, z, eng):
-            zi = slice(z * 1024, (z + 1) * 1024)
-            zo = slice(2048 + z * 1024, 2048 + (z + 1) * 1024)
+        def x_sq(b, z, n, eng):
+            zi = slice(z * 1024, (z + n) * 1024)
+            zo = slice(2048 + z * 1024, 2048 + (z + n) * 1024)
             if eng == "S":
                 nc.scalar.activation(out=xg[b][:, zo], in_=xg[b][:, zi], func=ACT.Square)
             elif eng == "V":
                 nc.vector.tensor_tensor(out=xg[b][:, zo], in0=xg[b][:, zi], in1=xg[b][:, zi], op=ALU.mult)
             else:
-                nc.gpsimd.tensor_tensor(out=xg[b][:, zo], in0=xg[b][:, zi], in1=xg[b][:, zi], op=ALU.mult)
+                for c in range(z * 1024, (z + n) * 1024, 512):
+                    nc.gpsimd.tensor_tensor(
+                        out=xg[b][:, 2048 + c : 2048 + c + 512], in0=xg[b][:, c : c + 512], in1=xg[b][:, c : c + 512],
+                        op=ALU.mult,
+                    )
 
-        def x_qt(b, kind):
-            nc.vector.quantize_mx(
-                out=xq[b][:, kind * 512 : (kind + 1) * 512].bitcast(FP8X4),
-                scales=xs[b][:, kind * 512 : (kind + 1) * 512],
-                in_=xg[b][:, kind * 2048 : (kind + 1) * 2048],
+        def x_qt(b):
+            xq[b] = xqp.tile([P, 1024], U32, name="xq", tag="xq", align_bytes=64)
+            xs[b] = xqp.tile([P, 1024], U8, name="xs", tag="xs", align_bytes=64)
+            nc.vector.quantize_mx(out=xq[b][:].bitcast(FP8X4), scales=xs[b][:], in_=xg[b][:])
+
+        def mx_pair(dst, l1, l1s, r1, r1s, l2, l2s, r2, r2s):
+            nc.tensor.matmul_mx(
+                out=dst, lhsT=l1.bitcast(FP8X4), lhsT_scale=l1s, rhs=r1.bitcast(FP8X4), rhs_scale=r1s,
+                start=True, stop=False,
+            )
+            nc.tensor.matmul_mx(
+                out=dst, lhsT=l2.bitcast(FP8X4), lhsT_scale=l2s, rhs=r2.bitcast(FP8X4), rhs_scale=r2s,
+                start=False, stop=True,
+            )
+
+        def m_t(b, jj, h=0):
+            if jj == 0:
+                s_t[(b, h)] = stp.tile([P, 4 * 512], F32, name="s_t", tag="s_t")
+            jc = slice(h * HC + jj * P, h * HC + (jj + 1) * P)
+            pt[(b, jj, h)] = bank("pt", "pb")
+            mx_pair(
+                pt[(b, jj, h)][:], w1c[:, jc], w1s[:, jc], xq[b][:, 512:1024], xs[b][:, 512:1024],
+                w2c[:, jc], w2s[:, jc], xq[b][:, 0:512], xs[b][:, 0:512],
+            )
+
+        def e_v(b, jj, h=0):
+            nc.scalar.activation(
+                out=s_t[(b, h)][:, jj * 512 : (jj + 1) * 512], in_=pt[(b, jj, h)][:], func=ACT.Identity,
+                bias=gcol[h][:, jj : jj + 1], scale=1.0,
             )
 
         with tc.tile_pool(name="pro", bufs=1) as pro:
-            d_sb = pro.tile([P, CT * DIM], BF16, name="d_sb", tag="d_sb")
-            c_sb = pro.tile([P, CT * DIM], BF16, name="c_sb", tag="c_sb")
+            d_sb = pro.tile([P, CT * DIM], BF16, name="d_sb", tag="d_sb", align_bytes=64)
+            c_sb = pro.tile([P, CT * DIM], BF16, name="c_sb", tag="c_sb", align_bytes=64)
             for src_v, dst_t in ((d_v, d_sb), (c_v, c_sb)):
                 for h in range(2):
                     cols = slice(h * 4 * DIM, (h + 1) * 4 * DIM)
                     nc.sync.dma_start(
                         out=dst_t[:, cols].rearrange("p (j d) -> p j d", j=4), in_=src_v[:, 4 * h : 4 * h + 4, :]
                     )
-            for c in range(5):
+            for t0, t1 in ((0, 4), (4, 12), (12, 20), (20, 28), (28, 36), (36, 40)):
                 nc.sync.dma_start(
-                    out=x_sb[:, c * 8 * DIM : (c + 1) * 8 * DIM].rearrange("p (t d) -> p t d", t=8),
-                    in_=x_v[:, 8 * c : 8 * c + 8, :],
+                    out=x_sb[:, t0 * DIM : t1 * DIM].rearrange("p (t d) -> p t d", t=t1 - t0), in_=x_v[:, t0:t1, :]
                 )
             d_i = d_sb[:].bitcast(I32)
             d_w = d_sb[:].bitcast(F32)
             c_w = c_sb[:].bitcast(F32)
             cg = pro.tile([P, CLS * 4], BF16, name="cg", tag="cg")
             cg_w = cg[:].bitcast(F32)
-            w1g = pro.tile([P, CLS * 4], BF16, name="w1g", tag="w1g", align_bytes=64)
-            w2g = pro.tile([P, CLS * 4], BF16, name="w2g", tag="w2g", align_bytes=64)
+            w1g = d_sb
+            w2g = c_sb
             lnr = [pro.tile([P, 4 * HC], F32, name="lnr%d" % h, tag="lnr%d" % h) for h in range(2)]
             dv = [pro.tile([P, 4 * HC], F32, name="dv%d" % h, tag="dv%d" % h) for h in range(2)]
-            csq = [pro.tile([P, 4 * HC], F32, name="csq%d" % h, tag="csq%d" % h) for h in range(2)]
+            cc = [pro.tile([P, 4 * HC], F32, name="cc", tag="cc")] * 2
             d_t = {}
             c_t = {}
-            g_p = {}
+            q_a = {}
 
             def p_and(h):
                 words = slice(h * 1024, (h + 1) * 1024)
@@ -184,10 +219,10 @@ def tile_axis_aligned_gmm_layer_t_kernel(tc, x, centers, D, out):
                 )
 
             def p_ctr(h, pr):
-                c_t[(h, pr)] = bank("cT", "pc" if h == 0 else "pd")
+                c_t[(h, pr)] = bank("cT", "pc")
                 for jj in range(2):
+                    src = (4 * h + 2 * pr + jj) * 256
                     for u in range(2):
-                        src = (4 * h + 2 * pr + jj) * 256
                         dst = (2 * jj + u) * P
                         nc.tensor.transpose(
                             out=c_t[(h, pr)][:, dst : dst + P], in_=c_w[:, src + u : src + 256 : 2], identity=ident[:]
@@ -200,64 +235,42 @@ def tile_axis_aligned_gmm_layer_t_kernel(tc, x, centers, D, out):
                     in_=c_t[(h, pr)][:].rearrange("p (j u r) -> p j r u", j=2, u=2),
                 )
 
-            def p_csq(h, eng):
-                cg_t = cg[:, h * 4 * HC : (h + 1) * 4 * HC].rearrange("p (r t) -> p t r", t=4)
-                cs_t = csq[h][:].rearrange("p (t r) -> p t r", t=4)
-                if eng == "V":
-                    nc.vector.tensor_tensor(out=cs_t, in0=cg_t, in1=cg_t, op=ALU.mult)
-                elif eng == "S":
-                    nc.scalar.activation(out=cs_t, in_=cg_t, func=ACT.Square)
-                else:
-                    nc.gpsimd.tensor_tensor(out=cs_t, in0=cg_t, in1=cg_t, op=ALU.mult)
+            def f_tr(t, h, pc):
+                return t[h][:].rearrange("p (t r) -> p t r", t=4)[:, :, pc * 256 : (pc + 1) * 256]
 
-            def p_gl(h, t):
-                if t == 0:
-                    g_p[h] = bank("gP", "pa")
-                nc.tensor.matmul(
-                    out=g_p[h][:], lhsT=half_c[:], rhs=lnr[h][:, t * HC : (t + 1) * HC], start=(t == 0), stop=False
-                )
+            def f_rt(t, h, pc):
+                return t[h][:].rearrange("p (t r) -> p r t", t=4)[:, pc * 256 : (pc + 1) * 256, :]
+
+            def g_cols(h, pc):
+                return slice((h * HC + pc * 256) * 4, (h * HC + (pc + 1) * 256) * 4)
 
             def p_exp(h, pc):
-                rr = slice(pc * 256, (pc + 1) * 256)
                 nc.scalar.activation(
-                    out=dv[h][:].rearrange("p (t r) -> p t r", t=4)[:, :, rr],
-                    in_=lnr[h][:].rearrange("p (t r) -> p t r", t=4)[:, :, rr],
-                    func=ACT.Exp,
-                    scale=-1.0,
-                    bias=lninv[:, 0:1],
+                    out=f_tr(dv, h, pc), in_=f_tr(lnr, h, pc), func=ACT.Exp, scale=-1.0, bias=lninv[:, 0:1]
                 )
 
             def p_w1(h, pc, eng):
-                rr = slice(pc * 256, (pc + 1) * 256)
-                gcols = slice((h * HC + pc * 256) * 4, (h * HC + (pc + 1) * 256) * 4)
-                if eng == "S":
-                    nc.scalar.activation(
-                        out=w1g[:, gcols].rearrange("p (r t) -> p r t", t=4),
-                        in_=dv[h][:].rearrange("p (t r) -> p r t", t=4)[:, rr, :],
-                        func=ACT.Copy,
-                        scale=0.5,
-                    )
-                    return
-                e = nc.gpsimd if eng == "G" else nc.vector
-                e.tensor_scalar(
-                    out=w1g[:, gcols].rearrange("p (r t) -> p r t", t=4),
-                    in0=dv[h][:].rearrange("p (t r) -> p r t", t=4)[:, rr, :],
-                    scalar1=0.5,
-                    scalar2=0.0,
-                    op0=ALU.mult,
-                    op1=ALU.add,
+                o_ap = w1g[:, g_cols(h, pc)].rearrange("p (r t) -> p r t", t=4)
+                if eng == "V":
+                    nc.vector.tensor_scalar_mul(out=o_ap, in0=f_rt(dv, h, pc), scalar1=0.5)
+                else:
+                    nc.scalar.activation(out=o_ap, in_=f_rt(dv, h, pc), func=ACT.Copy, scale=0.5)
+
+            def p_cd(h, pc):
+                nc.vector.tensor_tensor(
+                    out=f_tr(dv, h, pc), in0=f_tr(dv, h, pc),
+                    in1=cg[:, g_cols(h, pc)].rearrange("p (r t) -> p t r", t=4), op=ALU.mult,
                 )
 
             def p_w2(h, pc):
-                rr = slice(pc * 256, (pc + 1) * 256)
-                gcols = slice((h * HC + pc * 256) * 4, (h * HC + (pc + 1) * 256) * 4)
-                nc.vector.scalar_tensor_tensor(
-                    out=w2g[:, gcols].rearrange("p (r t) -> p r t", t=4),
-                    in0=dv[h][:].rearrange("p (t r) -> p r t", t=4)[:, rr, :],
-                    scalar=-1.0,
-                    in1=cg[:, gcols].rearrange("p (r t) -> p r t", t=4),
-                    op0=ALU.mult,
-                    op1=ALU.mult,
+                nc.vector.tensor_scalar_mul(
+                    out=w2g[:, g_cols(h, pc)].rearrange("p (r t) -> p r t", t=4), in0=f_rt(dv, h, pc), scalar1=-1.0
+                )
+
+            def p_ccd(h, pc):
+                nc.vector.tensor_tensor(
+                    out=f_tr(cc, h, pc), in0=f_tr(dv, h, pc),
+                    in1=cg[:, g_cols(h, pc)].rearrange("p (r t) -> p t r", t=4), op=ALU.mult,
                 )
 
             def p_qw(h, which):
@@ -268,98 +281,42 @@ def tile_axis_aligned_gmm_layer_t_kernel(tc, x, centers, D, out):
                 else:
                     nc.vector.quantize_mx(out=w2c[:, hc].bitcast(FP8X4), scales=w2s[:, hc], in_=w2g[:, hg])
 
-            def p_q(h, t, eng):
-                ts = slice(t * HC, (t + 1) * HC)
-                e = nc.gpsimd if eng == "G" else nc.vector
-                e.tensor_tensor(out=csq[h][:, ts], in0=dv[h][:, ts], in1=csq[h][:, ts], op=ALU.mult)
-
-            def p_gq(h, t):
-                ts = slice(t * HC, (t + 1) * HC)
-                nc.tensor.matmul(out=g_p[h][:], lhsT=half_c[:], rhs=csq[h][:, ts], start=False, stop=(t == 3))
-
-            def p_gb(h):
-                nc.scalar.copy(out=g_b[:, h * HC : (h + 1) * HC], in_=g_p[h][:])
-
-            def p_gcol():
-                g_t = bank("gT", "pb")
-                for jj in range(4):
-                    nc.tensor.transpose(
-                        out=g_t[:, jj * P : (jj + 1) * P], in_=g_b[:, jj * P : (jj + 1) * P], identity=ident[:]
-                    )
-                nc.vector.tensor_copy(
-                    out=gcol[:].rearrange("p (j o) -> p j o", o=1),
-                    in_=g_t[:].rearrange("p (j r) -> p j r", j=4)[:, :, 0:1],
-                )
-
-            glcol = pro.tile([P, 4], F32, name="glcol", tag="glcol")
-            gl_b = pro.tile([P, HC], F32, name="gl_b", tag="gl_b")
-            c2col = [pro.tile([P, 4], F32, name="c2col%d" % h, tag="c2col%d" % h) for h in range(2)]
-            c2h = pro.tile([P, 4], F32, name="c2h", tag="c2h")
-            q_a = {}
-
-            def p_gl2(h, t):
-                if t == 0:
-                    g_p[h] = bank("gP", "pa")
-                nc.tensor.matmul(
-                    out=g_p[h][:], lhsT=half_c[:], rhs=lnr[h][:, t * HC : (t + 1) * HC], start=(t == 0), stop=(t == 3)
-                )
-
-            def p_glc():
-                nc.scalar.copy(out=g_b[:, 0:HC], in_=g_p[0][:])
-                g_t = bank("gT", "pa")
-                for jj in range(4):
-                    nc.tensor.transpose(
-                        out=g_t[:, jj * P : (jj + 1) * P], in_=g_b[:, jj * P : (jj + 1) * P], identity=ident[:]
-                    )
-                nc.scalar.copy(
-                    out=glcol[:].rearrange("p (j o) -> p j o", o=1),
-                    in_=g_t[:].rearrange("p (j r) -> p j r", j=4)[:, :, 0:1],
-                )
-
-            def p_glb():
-                nc.scalar.copy(out=gl_b[:], in_=g_p[1][:])
-
-            def p_qp(h, pc, eng):
-                rr = slice(pc * 256, (pc + 1) * 256)
-                e = nc.gpsimd if eng == "G" else nc.vector
-                e.tensor_tensor(
-                    out=csq[h][:].rearrange("p (t r) -> p t r", t=4)[:, :, rr],
-                    in0=dv[h][:].rearrange("p (t r) -> p t r", t=4)[:, :, rr],
-                    in1=csq[h][:].rearrange("p (t r) -> p t r", t=4)[:, :, rr],
-                    op=ALU.mult,
-                )
-
-            def p_at(h, jj, tag):
+            def p_at(h, jj):
                 if jj == 0:
-                    q_a[h] = bank("qA", tag)
-                for t in range(4):
+                    q_a[h] = bank("qA", "pa")
+                parts = [(lnr, t) for t in range(4)] + [(cc, t) for t in range(4)]
+                for z in range(8):
+                    src, t = parts[z]
                     nc.tensor.matmul(
                         out=q_a[h][:, jj * P : (jj + 1) * P],
-                        lhsT=csq[h][:, t * HC + jj * P : t * HC + (jj + 1) * P],
+                        lhsT=src[h][:, t * HC + jj * P : t * HC + (jj + 1) * P],
                         rhs=ident[:],
                         is_transpose=True,
-                        start=(t == 0),
-                        stop=(t == 3),
+                        start=(z == 0),
+                        stop=(z == 7),
                     )
 
             def p_c2(h):
                 nc.vector.tensor_reduce(
                     out=c2col[h][:], in_=q_a[h][:].rearrange("p (j r) -> p j r", j=4), axis=AX.X, op=ALU.add
                 )
-                if h == 0:
-                    nc.vector.scalar_tensor_tensor(
-                        out=gcol[:], in0=c2col[0][:], scalar=0.5, in1=glcol[:], op0=ALU.mult, op1=ALU.add
-                    )
-                else:
-                    nc.vector.tensor_scalar_mul(out=c2h[:], in0=c2col[1][:], scalar1=0.5)
 
-            def p_gb2(tag):
-                b_b = bank("bB", tag)
+            def p_gcol(h):
+                nc.scalar.mul(gcol[h][:], c2col[h][:], 0.5)
+
+            b_b = {}
+
+            def p_gbt():
+                b_b[0] = bank("bB", "pa")
                 for jj in range(4):
                     nc.tensor.transpose(
-                        out=b_b[:, jj * P : (jj + 1) * P], in_=c2h[:, jj : jj + 1].to_broadcast([P, P]), identity=ident[:]
+                        out=b_b[0][:, jj * P : (jj + 1) * P],
+                        in_=gcol[1][:, jj : jj + 1].to_broadcast([P, P]),
+                        identity=ident[:],
                     )
-                nc.vector.tensor_tensor(out=g_b[:, HC:CLS], in0=b_b[:], in1=gl_b[:], op=ALU.add)
+
+            def p_gbc():
+                nc.scalar.copy(out=g_b[:], in_=b_b[0][:])
 
             p_and(0)
             p_and(1)
@@ -373,111 +330,83 @@ def tile_axis_aligned_gmm_layer_t_kernel(tc, x, centers, D, out):
                 for pr in range(2):
                     p_ctr(h, pr)
                     p_cgc(h, pr)
-            p_csq(0, "V")
-            for t in range(4):
-                p_gl2(0, t)
-            x_tr(0, 0)
-            x_tr(0, 1)
-            p_csq(1, "V")
-            for t in range(4):
-                p_gl2(1, t)
+            for half in range(2):
+                x_tr(0, half)
+                x_cp(0, half, "V")
+            x_sq(0, 0, 2, "V")
+            x_tr(1, 0)
+            x_tr(1, 1)
+            x_qt(0)
             for h in range(2):
                 for pc in range(2):
                     p_exp(h, pc)
-                    p_w1(h, pc, "G")
-                    p_w2(h, pc)
-                p_qw(h, 2)
-                if h == 0:
-                    p_qp(0, 0, "V")
-                    p_qp(0, 1, "V")
-            p_glc()
-            p_glb()
-            for jj in range(4):
-                p_at(0, jj, "pc")
-            p_qp(1, 0, "V")
-            p_qp(1, 1, "V")
-            x_cp(0, 0, "S")
-            x_cp(0, 1, "S")
-            x_tr(1, 0)
-            x_tr(1, 1)
-            p_c2(0)
-            x_sq(0, 0, "S")
-            x_sq(0, 1, "S")
-            x_cp(1, 0, "S")
-            x_cp(1, 1, "S")
-            for jj in range(4):
-                p_at(1, jj, "pc")
-            x_qt(0, 0)
-            p_c2(1)
-            p_gb2("pc")
+            for pc in range(2):
+                p_w1(0, pc, "V")
+                p_cd(0, pc)
+            for pc in range(2):
+                p_w2(0, pc)
             p_qw(0, 1)
-            p_qw(1, 1)
+            p_qw(0, 2)
+            p_w1(1, 0, "S")
+            p_w1(1, 1, "S")
+            for half in range(2):
+                x_cp(1, half, "S")
+            m_t(0, 0)
+            m_t(0, 1)
             x_tr(2, 0)
             x_tr(2, 1)
-            x_sq(1, 0, "S")
-            x_sq(1, 1, "S")
-            x_cp(2, 0, "S")
-            x_cp(2, 1, "S")
+            x_sq(1, 0, 2, "S")
+            for half in range(2):
+                x_cp(2, half, "S")
+            x_sq(2, 0, 2, "S")
+            for pc in range(2):
+                p_ccd(0, pc)
+                p_at(0, 2 * pc)
+                p_at(0, 2 * pc + 1)
+            p_cd(1, 0)
+            p_cd(1, 1)
+            x_qt(1)
+            p_c2(0)
+            p_gcol(0)
+            e_v(0, 0)
+            e_v(0, 1)
             x_tr(3, 0)
             x_tr(3, 1)
-            x_cp(3, 0, "S")
-            x_cp(3, 1, "S")
-            x_sq(2, 0, "G")
-            x_sq(2, 1, "G")
-            x_sq(3, 0, "G")
-            x_sq(3, 1, "G")
-            x_qt(0, 1)
-            x_qt(1, 0)
-            x_qt(1, 1)
-            x_qt(2, 0)
-            x_qt(3, 0)
+            for pc in range(2):
+                m_t(0, 2 + pc)
+                e_v(0, 2 + pc)
+            for pc in range(2):
+                p_ccd(1, pc)
+                p_at(1, 2 * pc)
+                p_at(1, 2 * pc + 1)
+            for half in range(2):
+                x_cp(3, half, "S")
+            for pc in range(2):
+                p_w2(1, pc)
+            p_qw(1, 1)
+            p_c2(1)
+            p_gcol(1)
+            p_gbt()
+            p_gbc()
+            p_qw(1, 2)
+            x_sq(3, 0, 2, "S")
+            x_qt(2)
 
-        work = ctx.enter_context(tc.tile_pool(name="work", bufs=O4_BUFS))
-        stp = ctx.enter_context(tc.tile_pool(name="stp", bufs=ST_BUFS))
-        o4 = {}
-        s_t = {}
-        pt = {}
-        acc = {}
-        st = {}
+        o2p = ctx.enter_context(tc.tile_pool(name="o2p", bufs=O2_BUFS))
+        o2 = {}
         dmin = {}
         nmin = {}
+        nmin0 = {}
         sums = {}
         rec = {}
 
-        def mx_pair(dst, l1, l1s, r1, r1s, l2, l2s, r2, r2s):
-            nc.tensor.matmul_mx(
-                out=dst, lhsT=l1.bitcast(FP8X4), lhsT_scale=l1s, rhs=r1.bitcast(FP8X4), rhs_scale=r1s,
-                start=True, stop=False,
-            )
-            nc.tensor.matmul_mx(
-                out=dst, lhsT=l2.bitcast(FP8X4), lhsT_scale=l2s, rhs=r2.bitcast(FP8X4), rhs_scale=r2s,
-                start=False, stop=True,
-            )
+        def o_cols(b, i, c0, c1):
+            return o2[(b, i // 2)][:, (i % 2) * CLS + c0 : (i % 2) * CLS + c1]
 
-        def m_t(b, jj):
-            if jj == 0:
-                s_t[b] = stp.tile([P, 4 * 512], F32, name="s_t", tag="s_t")
-            jc = slice(jj * P, (jj + 1) * P)
-            pt[(b, jj)] = bank("pt", "pb")
-            mx_pair(
-                pt[(b, jj)][:], w1c[:, jc], w1s[:, jc], xq[b][:, 512:1024], xs[b][:, 512:1024],
-                w2c[:, jc], w2s[:, jc], xq[b][:, 0:512], xs[b][:, 0:512],
-            )
-
-        def e_v(b, jj, eng):
-            if eng == "S":
-                nc.scalar.activation(
-                    out=s_t[b][:, jj * 512 : (jj + 1) * 512], in_=pt[(b, jj)][:], func=ACT.Identity,
-                    bias=gcol[:, jj : jj + 1], scale=1.0,
-                )
-            else:
-                nc.vector.tensor_scalar_add(
-                    out=s_t[b][:, jj * 512 : (jj + 1) * 512], in0=pt[(b, jj)][:], scalar1=gcol[:, jj : jj + 1]
-                )
+        def col(t, b, i):
+            return t[(b, i // 2)][:, i % 2 : i % 2 + 1]
 
         def m_d(b, i):
-            if i == 0:
-                o4[b] = work.tile([P, 4 * CLS], F32, name="o4", tag="o4")
             rc = slice(i * P, (i + 1) * P)
             rc2 = slice(512 + i * P, 512 + (i + 1) * P)
             hc = slice(HC, CLS)
@@ -488,114 +417,136 @@ def tile_axis_aligned_gmm_layer_t_kernel(tc, x, centers, D, out):
             )
 
         def a_d(b, i):
-            nc.vector.tensor_tensor(
-                out=o4[b][:, i * CLS + HC : (i + 1) * CLS], in0=acc[(b, i)][:], in1=g_b[:, HC:CLS], op=ALU.add
-            )
+            if i % 2 == 0:
+                o2[(b, i // 2)] = o2p.tile([P, 2 * CLS], F32, name="o2", tag="o2")
+            nc.vector.tensor_tensor(out=o_cols(b, i, HC, CLS), in0=acc[(b, i)][:], in1=g_b[:], op=ALU.add)
 
-        def d_m(b):
-            dmin[b] = small.tile([P, 4], F32, name="dmin", tag="dmin")
-            nmin[b] = small.tile([P, 4], F32, name="nmin", tag="nmin")
+        def d_m(b, pr):
+            dmin[(b, pr)] = small.tile([P, 2], F32, name="dmin", tag="dmin")
+            nmin[(b, pr)] = small.tile([P, 2], F32, name="nmin", tag="nmin")
             nc.vector.tensor_reduce(
-                out=dmin[b][:], in_=o4[b][:].rearrange("p (i k) -> p i k", i=4)[:, :, HC:CLS], axis=AX.X, op=ALU.min
+                out=dmin[(b, pr)][:], in_=o2[(b, pr)][:].rearrange("p (i k) -> p i k", i=2)[:, :, HC:CLS],
+                axis=AX.X, op=ALU.min,
             )
 
-        def b_t(b, i):
-            st[(b, i)] = bank("st", "pa")
+        def b_t(b, i, h=0):
+            st[(b, i, h)] = bank("st", "pa" if h == 0 else "pc")
             for jj in range(4):
                 nc.tensor.transpose(
-                    out=st[(b, i)][:, jj * P : (jj + 1) * P],
-                    in_=s_t[b][:, jj * 512 + i * P : jj * 512 + (i + 1) * P],
+                    out=st[(b, i, h)][:, jj * P : (jj + 1) * P],
+                    in_=s_t[(b, h)][:, jj * 512 + i * P : jj * 512 + (i + 1) * P],
                     identity=ident[:],
                 )
 
-        def e_m(b, i):
+        def e_m(b, i, h=0):
+            prev = dmin if h == 0 else nmin0
+            now = nmin0 if (h == 0 and b in FULL) else nmin
             nc.vector.tensor_scalar(
-                out=o4[b][:, i * CLS : i * CLS + HC], in0=st[(b, i)][:], scalar1=0.0, scalar2=dmin[b][:, i : i + 1],
-                op0=ALU.add, op1=ALU.min, accum_out=nmin[b][:, i : i + 1],
+                out=o_cols(b, i, h * HC, (h + 1) * HC), in0=st[(b, i, h)][:], scalar1=0.0,
+                scalar2=None if (h == 0 and b in FULL) else col(prev, b, i),
+                op0=ALU.add, op1=ALU.min, accum_out=col(now, b, i),
             )
 
         def e_x(b, i):
-            if i == 0:
-                sums[b] = small.tile([P, 4], F32, name="sums", tag="sums")
-                rec[b] = small.tile([P, 4], F32, name="rec", tag="rec")
-            ic = slice(i * CLS, (i + 1) * CLS)
+            if i % 2 == 0:
+                sums[(b, i // 2)] = small.tile([P, 2], F32, name="sums", tag="sums")
+                rec[(b, i // 2)] = small.tile([P, 2], F32, name="rec", tag="rec")
             nc.scalar.activation(
-                out=o4[b][:, ic], in_=o4[b][:, ic], func=ACT.Exp, bias=nmin[b][:, i : i + 1], scale=-1.0,
-                accum_out=sums[b][:, i : i + 1],
+                out=o_cols(b, i, 0, CLS), in_=o_cols(b, i, 0, CLS), func=ACT.Exp, bias=col(nmin, b, i), scale=-1.0,
+                accum_out=col(sums, b, i),
             )
 
-        def r_c(b):
-            nc.vector.reciprocal(out=rec[b][:], in_=sums[b][:])
+        def r_c(b, pr):
+            nc.vector.reciprocal(out=rec[(b, pr)][:], in_=sums[(b, pr)][:])
 
         def r_c1(b, i):
-            nc.vector.reciprocal(out=rec[b][:, i : i + 1], in_=sums[b][:, i : i + 1])
+            nc.vector.reciprocal(out=col(rec, b, i), in_=col(sums, b, i))
 
         def s_c(b, i, eng="G"):
-            ic = slice(i * CLS, (i + 1) * CLS)
             if eng == "V":
-                nc.vector.tensor_scalar_mul(
-                    out=o4[b][:, ic], in0=o4[b][:, ic], scalar1=rec[b][:, i : i + 1]
-                )
-            else:
+                nc.vector.tensor_scalar_mul(out=o_cols(b, i, 0, CLS), in0=o_cols(b, i, 0, CLS), scalar1=col(rec, b, i))
+                return
+            for c0 in range(0, CLS, SC_COLS):
+                ap = o_cols(b, i, c0, c0 + SC_COLS)
                 nc.gpsimd.tensor_scalar(
-                    out=o4[b][:, ic], in0=o4[b][:, ic], scalar1=rec[b][:, i : i + 1], scalar2=0.0,
-                    op0=ALU.mult, op1=ALU.add,
+                    out=ap, in0=ap, scalar1=col(rec, b, i), scalar2=0.0, op0=ALU.mult, op1=ALU.add
                 )
 
         def store1(b, i):
-            nc.sync.dma_start(out=out_v[:, 4 * b + i, :], in_=o4[b][:, i * CLS : (i + 1) * CLS])
+            nc.sync.dma_start(out=out_v[:, 4 * b + i, :], in_=o_cols(b, i, 0, CLS))
 
-        def s_t_ore(b, pr):
+        def store2(b, pr):
             t0 = 4 * b + 2 * pr
             nc.sync.dma_start(
-                out=out_v[:, t0 : t0 + 2, :],
-                in_=o4[b][:].rearrange("p (i k) -> p i k", i=4)[:, 2 * pr : 2 * pr + 2, :],
+                out=out_v[:, t0 : t0 + 2, :], in_=o2[(b, pr)][:].rearrange("p (i k) -> p i k", i=2)
             )
 
-        def sched(n):
-            todo = {}
-            for key in OFF:
-                m = n - OFF[key]
-                todo[key] = (m // 4, m % 4) if 0 <= m < 4 * NB else None
-            return todo
+        def tile_at(n, off):
+            m = n - off
+            return (m // 4, m % 4) if 0 <= m < NT else (-1, 0)
 
-        for n in range(N_LO, 4 * NB + N_HI + 1):
-            td = sched(n)
-            if td["bt"]:
-                b_t(*td["bt"])
-            if td["xtr"] and td["xtr"][1] % 2 == 0 and td["xtr"][0] >= PRE:
-                x_tr(td["xtr"][0], td["xtr"][1] // 2)
-            if td["mt"]:
-                m_t(*td["mt"])
-            if td["md"]:
-                m_d(*td["md"])
-            if td["em"]:
-                e_m(*td["em"])
-            if td["ev"]:
-                e_v(td["ev"][0], td["ev"][1], "S")
-            if td["ad"]:
-                a_d(*td["ad"])
-                if td["ad"][1] == 3:
-                    d_m(td["ad"][0])
-            if td["ex"]:
-                e_x(*td["ex"])
-            if td["xcp"] and td["xcp"][1] % 2 == 0 and td["xcp"][0] >= PRE:
-                x_cp(td["xcp"][0], td["xcp"][1] // 2, "S")
-            if td["xq0"] and td["xq0"][1] == 0 and td["xq0"][0] >= PRE:
-                x_qt(td["xq0"][0], 0)
-            if td["rc"] and td["rc"][0] >= NB - LASTV:
-                r_c1(*td["rc"])
-                s_c(td["rc"][0], td["rc"][1], "V")
-                store1(*td["rc"])
-            elif td["rc"] and td["rc"][1] == 3:
-                r_c(td["rc"][0])
-            if td["sc"] and td["sc"][0] < NB - LASTV:
-                s_c(*td["sc"])
-                if td["sc"][0] >= NB - LAST1:
-                    store1(*td["sc"])
-                elif td["sc"][1] % 2 == 1:
-                    s_t_ore(td["sc"][0], td["sc"][1] // 2)
-            if td["xsq"] and td["xsq"][1] % 2 == 0 and td["xsq"][0] >= PRE:
-                x_sq(td["xsq"][0], td["xsq"][1] // 2, SQM[td["xsq"][0]][td["xsq"][1] // 2])
-            if td["xq1"] and td["xq1"][1] == 0 and td["xq1"][0] >= PRE_Q1:
-                x_qt(td["xq1"][0], 1)
+        for n in range(MD, NT + SC + 1):
+            b, i = tile_at(n, BT)
+            if b >= 0:
+                b_t(b, i)
+                if b in FULL:
+                    b_t(b, i, 1)
+            b, i = tile_at(n, XTR)
+            if b >= X_PRO and i % 2 == 0:
+                x_tr(b, i // 2)
+            b, i = tile_at(n, MD)
+            if b >= 0 and b not in FULL:
+                m_d(b, i)
+            b, i = tile_at(n, MT)
+            if b >= M_PRO:
+                m_t(b, i)
+                if b in FULL:
+                    m_t(b, i, 1)
+            b, i = tile_at(n, 0)
+            if b >= 0:
+                if b in FULL:
+                    if i % 2 == 0:
+                        o2[(b, i // 2)] = o2p.tile([P, 2 * CLS], F32, name="o2", tag="o2")
+                        nmin0[(b, i // 2)] = small.tile([P, 2], F32, name="nmin0", tag="nmin0")
+                        nmin[(b, i // 2)] = small.tile([P, 2], F32, name="nmin", tag="nmin")
+                    e_m(b, i)
+                    e_m(b, i, 1)
+                else:
+                    e_m(b, i)
+            b, i = tile_at(n, EV)
+            if b >= M_PRO:
+                e_v(b, i)
+                if b in FULL:
+                    e_v(b, i, 1)
+            b, i = tile_at(n, AD)
+            if b >= 0 and b not in FULL:
+                a_d(b, i)
+            b, i = tile_at(n, AD + 1)
+            if b >= 0 and i % 2 == 1 and b not in FULL:
+                d_m(b, i // 2)
+            b, i = tile_at(n, 0)
+            if b >= 0:
+                e_x(b, i)
+            b, i = tile_at(n, XCP)
+            if b >= X_PRO and i % 2 == 0:
+                x_cp(b, i // 2, "S")
+            b, i = tile_at(n, XSQ)
+            if b >= X_PRO and i % 2 == 0:
+                x_sq(b, i // 2, 1, SQE[i // 2])
+            b, i = tile_at(n, XQ)
+            if b >= Q_PRO and i == 0:
+                x_qt(b)
+            b, i = tile_at(n, RC)
+            if b >= NB - LASTV:
+                r_c1(b, i)
+                s_c(b, i, "V")
+                store1(b, i)
+            elif b >= 0 and i % 2 == 1:
+                r_c(b, i // 2)
+            b, i = tile_at(n, SC)
+            if 0 <= b < NB - LASTV:
+                s_c(b, i)
+                if b >= NB - LASTV - 1:
+                    store1(b, i)
+                elif i % 2 == 1:
+                    store2(b, i // 2)

@@ -39,7 +39,7 @@ XQ = -9
 X_PRO = 4
 Q_PRO = 3
 M_PRO = 1
-SQE = "SV"
+SQE = "VGSG"
 LASTV = 1
 SC_COLS = 512
 O2_BUFS = 9
@@ -68,6 +68,14 @@ def tile_axis_aligned_gmm_layer_t_kernel(tc, x, centers, D, out):
         nc.scalar.activation(out=warm[:], in_=one[:], func=ACT.Ln)
         ident = const.tile([P, P], F32, name="ident", tag="ident")
         make_identity(nc, ident[:])
+
+        ones = const.tile([P, 512], BF16, name="ones", tag="ones")
+        nc.vector.memset(ones[:], 1.0)
+
+        def warm_up(count, rhs, tag):
+            wb = bank("wb", tag)
+            for z in range(count):
+                nc.tensor.matmul(out=wb[:], lhsT=ones[:, 0:P], rhs=rhs, start=True, stop=True)
 
         x_sb = const.tile([P, NT * DIM], BF16, name="x_sb", tag="x_sb")
         w1c = const.tile([P, CLS], U32, name="w1c", tag="w1c", align_bytes=64)
@@ -164,16 +172,26 @@ def tile_axis_aligned_gmm_layer_t_kernel(tc, x, centers, D, out):
         with tc.tile_pool(name="pro", bufs=1) as pro:
             d_sb = pro.tile([P, CT * DIM], BF16, name="d_sb", tag="d_sb", align_bytes=64)
             c_sb = pro.tile([P, CT * DIM], BF16, name="c_sb", tag="c_sb", align_bytes=64)
-            for src_v, dst_t in ((d_v, d_sb), (c_v, c_sb)):
-                for h in range(2):
-                    cols = slice(h * 4 * DIM, (h + 1) * 4 * DIM)
-                    nc.sync.dma_start(
-                        out=dst_t[:, cols].rearrange("p (j d) -> p j d", j=4), in_=src_v[:, 4 * h : 4 * h + 4, :]
-                    )
-            for t0, t1 in ((0, 4), (4, 12), (12, 20), (20, 28), (28, 36), (36, 40)):
+
+            def load_w(src_v, dst_t, h):
+                cols = slice(h * 4 * DIM, (h + 1) * 4 * DIM)
+                nc.sync.dma_start(
+                    out=dst_t[:, cols].rearrange("p (j d) -> p j d", j=4), in_=src_v[:, 4 * h : 4 * h + 4, :]
+                )
+
+            def load_x(t0, t1):
                 nc.sync.dma_start(
                     out=x_sb[:, t0 * DIM : t1 * DIM].rearrange("p (t d) -> p t d", t=t1 - t0), in_=x_v[:, t0:t1, :]
                 )
+
+            load_w(d_v, d_sb, 0)
+            load_w(d_v, d_sb, 1)
+            load_x(0, 4)
+            load_w(c_v, c_sb, 0)
+            load_w(c_v, c_sb, 1)
+            load_x(4, 8)
+            for t0 in range(8, NT, 8):
+                load_x(t0, t0 + 8)
             d_i = d_sb[:].bitcast(I32)
             d_w = d_sb[:].bitcast(F32)
             c_w = c_sb[:].bitcast(F32)
@@ -318,24 +336,34 @@ def tile_axis_aligned_gmm_layer_t_kernel(tc, x, centers, D, out):
             def p_gbc():
                 nc.scalar.copy(out=g_b[:], in_=b_b[0][:])
 
+            warm_up(11, ones[:], "pd")
             p_and(0)
             p_and(1)
             p_dtr(0)
             p_rho()
+            warm_up(2, ones[:], "pd")
             p_dtr(1)
             for h in range(2):
                 for u in range(2):
                     p_ln(h, u)
-            for h in range(2):
-                for pr in range(2):
-                    p_ctr(h, pr)
-                    p_cgc(h, pr)
+            warm_up(2, ones[:], "pd")
+            p_ctr(0, 0)
+            p_cgc(0, 0)
+            p_ctr(0, 1)
+            p_cgc(0, 1)
+            warm_up(2, ones[:], "pd")
             for half in range(2):
                 x_tr(0, half)
                 x_cp(0, half, "V")
+            warm_up(2, ones[:], "pa")
             x_sq(0, 0, 2, "V")
+            for pr in range(2):
+                p_ctr(1, pr)
+                p_cgc(1, pr)
+            warm_up(2, ones[:], "pa")
             x_tr(1, 0)
             x_tr(1, 1)
+            warm_up(4, xg[0][:, 2048:2560], "pa")
             x_qt(0)
             for h in range(2):
                 for pc in range(2):
@@ -345,33 +373,33 @@ def tile_axis_aligned_gmm_layer_t_kernel(tc, x, centers, D, out):
                 p_cd(0, pc)
             for pc in range(2):
                 p_w2(0, pc)
+            for pc in range(2):
+                warm_up(4, w1g[:, g_cols(0, pc)][:, 0:512], "pa")
             p_qw(0, 1)
             p_qw(0, 2)
             p_w1(1, 0, "S")
             p_w1(1, 1, "S")
             for half in range(2):
                 x_cp(1, half, "S")
-            m_t(0, 0)
-            m_t(0, 1)
+            x_sq(1, 0, 2, "S")
+            warm_up(2, w2g[:, g_cols(0, 1)][:, 0:512], "pa")
             x_tr(2, 0)
             x_tr(2, 1)
-            x_sq(1, 0, 2, "S")
             for half in range(2):
                 x_cp(2, half, "S")
             x_sq(2, 0, 2, "S")
             for pc in range(2):
+                m_t(0, pc)
                 p_ccd(0, pc)
                 p_at(0, 2 * pc)
                 p_at(0, 2 * pc + 1)
+            warm_up(3, ones[:], "pc")
             p_cd(1, 0)
             p_cd(1, 1)
-            x_qt(1)
             p_c2(0)
             p_gcol(0)
             e_v(0, 0)
             e_v(0, 1)
-            x_tr(3, 0)
-            x_tr(3, 1)
             for pc in range(2):
                 m_t(0, 2 + pc)
                 e_v(0, 2 + pc)
@@ -379,18 +407,23 @@ def tile_axis_aligned_gmm_layer_t_kernel(tc, x, centers, D, out):
                 p_ccd(1, pc)
                 p_at(1, 2 * pc)
                 p_at(1, 2 * pc + 1)
+                warm_up(2, ones[:], "pc")
+            x_tr(3, 0)
+            x_tr(3, 1)
             for half in range(2):
                 x_cp(3, half, "S")
+            warm_up(2, ones[:], "pc")
             for pc in range(2):
                 p_w2(1, pc)
             p_qw(1, 1)
+            p_qw(1, 2)
             p_c2(1)
             p_gcol(1)
             p_gbt()
             p_gbc()
-            p_qw(1, 2)
-            x_sq(3, 0, 2, "S")
+            x_qt(1)
             x_qt(2)
+            x_sq(3, 0, 2, "V")
 
         o2p = ctx.enter_context(tc.tile_pool(name="o2p", bufs=O2_BUFS))
         o2 = {}
@@ -532,7 +565,7 @@ def tile_axis_aligned_gmm_layer_t_kernel(tc, x, centers, D, out):
                 x_cp(b, i // 2, "S")
             b, i = tile_at(n, XSQ)
             if b >= X_PRO and i % 2 == 0:
-                x_sq(b, i // 2, 1, SQE[i // 2])
+                x_sq(b, i // 2, 1, SQE[(2 * b + i // 2) % len(SQE)])
             b, i = tile_at(n, XQ)
             if b >= Q_PRO and i == 0:
                 x_qt(b)

@@ -39,7 +39,7 @@ XQ = -9
 X_PRO = 4
 Q_PRO = 3
 M_PRO = 1
-SQE = "VGSG"
+SQE = "SV"
 LASTV = 1
 SC_COLS = 512
 O2_BUFS = 9
@@ -280,10 +280,12 @@ def tile_axis_aligned_gmm_layer_t_kernel(tc, x, centers, D, out):
                     in1=cg[:, g_cols(h, pc)].rearrange("p (r t) -> p t r", t=4), op=ALU.mult,
                 )
 
-            def p_w2(h, pc):
-                nc.vector.tensor_scalar_mul(
-                    out=w2g[:, g_cols(h, pc)].rearrange("p (r t) -> p r t", t=4), in0=f_rt(dv, h, pc), scalar1=-1.0
-                )
+            def p_w2(h, pc, eng):
+                o_ap = w2g[:, g_cols(h, pc)].rearrange("p (r t) -> p r t", t=4)
+                if eng == "V":
+                    nc.vector.tensor_scalar_mul(out=o_ap, in0=f_rt(dv, h, pc), scalar1=-1.0)
+                else:
+                    nc.scalar.activation(out=o_ap, in_=f_rt(dv, h, pc), func=ACT.Copy, scale=-1.0)
 
             def p_ccd(h, pc):
                 nc.vector.tensor_tensor(
@@ -336,26 +338,26 @@ def tile_axis_aligned_gmm_layer_t_kernel(tc, x, centers, D, out):
             def p_gbc():
                 nc.scalar.copy(out=g_b[:], in_=b_b[0][:])
 
-            warm_up(11, ones[:], "pd")
+            warm_up(11, ones[:], "pc")
             p_and(0)
             p_and(1)
             p_dtr(0)
             p_rho()
-            warm_up(2, ones[:], "pd")
+            warm_up(2, ones[:], "pc")
+            x_tr(0, 0)
+            x_cp(0, 0, "V")
             p_dtr(1)
+            warm_up(2, ones[:], "pc")
+            x_tr(0, 1)
+            x_cp(0, 1, "V")
             for h in range(2):
                 for u in range(2):
                     p_ln(h, u)
-            warm_up(2, ones[:], "pd")
             p_ctr(0, 0)
             p_cgc(0, 0)
             p_ctr(0, 1)
             p_cgc(0, 1)
             warm_up(2, ones[:], "pd")
-            for half in range(2):
-                x_tr(0, half)
-                x_cp(0, half, "V")
-            warm_up(2, ones[:], "pa")
             x_sq(0, 0, 2, "V")
             for pr in range(2):
                 p_ctr(1, pr)
@@ -372,7 +374,7 @@ def tile_axis_aligned_gmm_layer_t_kernel(tc, x, centers, D, out):
                 p_w1(0, pc, "V")
                 p_cd(0, pc)
             for pc in range(2):
-                p_w2(0, pc)
+                p_w2(0, pc, "V")
             for pc in range(2):
                 warm_up(4, w1g[:, g_cols(0, pc)][:, 0:512], "pa")
             p_qw(0, 1)
@@ -403,27 +405,26 @@ def tile_axis_aligned_gmm_layer_t_kernel(tc, x, centers, D, out):
             for pc in range(2):
                 m_t(0, 2 + pc)
                 e_v(0, 2 + pc)
-            for pc in range(2):
                 p_ccd(1, pc)
                 p_at(1, 2 * pc)
                 p_at(1, 2 * pc + 1)
-                warm_up(2, ones[:], "pc")
+            warm_up(2, ones[:], "pc")
             x_tr(3, 0)
             x_tr(3, 1)
-            for half in range(2):
-                x_cp(3, half, "S")
-            warm_up(2, ones[:], "pc")
-            for pc in range(2):
-                p_w2(1, pc)
             p_qw(1, 1)
-            p_qw(1, 2)
+            x_qt(1)
             p_c2(1)
+            p_w2(1, 0, "S")
             p_gcol(1)
+            p_w2(1, 1, "S")
+            warm_up(2, ones[:], "pc")
             p_gbt()
             p_gbc()
-            x_qt(1)
+            p_qw(1, 2)
+            for half in range(2):
+                x_cp(3, half, "S")
+            x_sq(3, 0, 2, "S")
             x_qt(2)
-            x_sq(3, 0, 2, "V")
 
         o2p = ctx.enter_context(tc.tile_pool(name="o2p", bufs=O2_BUFS))
         o2 = {}

@@ -30,6 +30,7 @@ EV = -5
 MD = -5
 AD = -4
 BT = -1
+EX = 0
 RC = 1
 SC = 3
 XTR = -17
@@ -69,14 +70,6 @@ def tile_axis_aligned_gmm_layer_t_kernel(tc, x, centers, D, out):
         ident = const.tile([P, P], F32, name="ident", tag="ident")
         make_identity(nc, ident[:])
 
-        ones = const.tile([P, 512], BF16, name="ones", tag="ones")
-        nc.vector.memset(ones[:], 1.0)
-
-        def warm_up(count, rhs, tag):
-            wb = bank("wb", tag)
-            for z in range(count):
-                nc.tensor.matmul(out=wb[:], lhsT=ones[:, 0:P], rhs=rhs, start=True, stop=True)
-
         x_sb = const.tile([P, NT * DIM], BF16, name="x_sb", tag="x_sb")
         w1c = const.tile([P, CLS], U32, name="w1c", tag="w1c", align_bytes=64)
         w2c = const.tile([P, CLS], U32, name="w2c", tag="w2c", align_bytes=64)
@@ -85,9 +78,8 @@ def tile_axis_aligned_gmm_layer_t_kernel(tc, x, centers, D, out):
         g_b = const.tile([P, HC], F32, name="g_b", tag="g_b")
         gcol = [const.tile([P, 4], F32, name="gcol%d" % h, tag="gcol%d" % h) for h in range(2)]
         c2col = [const.tile([P, 4], F32, name="c2col%d" % h, tag="c2col%d" % h) for h in range(2)]
-        a0 = const.tile([P, 1], F32, name="a0", tag="a0")
-        inv = const.tile([P, 1], F32, name="inv", tag="inv")
-        einv = const.tile([P, 1], F32, name="einv", tag="einv")
+        a0 = const.tile([P, 2], F32, name="a0", tag="a0")
+        inv = const.tile([P, 2], F32, name="inv", tag="inv")
         lninv = const.tile([P, 1], F32, name="lninv", tag="lninv")
         x_w = x_sb[:].bitcast(F32)
         x_v = x.rearrange("(p t) d -> p t d", t=NT)
@@ -104,8 +96,8 @@ def tile_axis_aligned_gmm_layer_t_kernel(tc, x, centers, D, out):
         acc = {}
         st = {}
 
-        def x_tr(b, half):
-            xt[(b, half)] = bank("xT", "pd")
+        def x_tr(b, half, tag):
+            xt[(b, half)] = bank("xT", tag)
             for i in range(2):
                 src = (4 * b + 2 * half + i) * 256
                 for u in range(2):
@@ -173,10 +165,9 @@ def tile_axis_aligned_gmm_layer_t_kernel(tc, x, centers, D, out):
             d_sb = pro.tile([P, CT * DIM], BF16, name="d_sb", tag="d_sb", align_bytes=64)
             c_sb = pro.tile([P, CT * DIM], BF16, name="c_sb", tag="c_sb", align_bytes=64)
 
-            def load_w(src_v, dst_t, h):
-                cols = slice(h * 4 * DIM, (h + 1) * 4 * DIM)
+            def load_w(src_v, dst_t, j0, j1):
                 nc.sync.dma_start(
-                    out=dst_t[:, cols].rearrange("p (j d) -> p j d", j=4), in_=src_v[:, 4 * h : 4 * h + 4, :]
+                    out=dst_t[:, j0 * DIM : j1 * DIM].rearrange("p (j d) -> p j d", j=j1 - j0), in_=src_v[:, j0:j1, :]
                 )
 
             def load_x(t0, t1):
@@ -184,30 +175,30 @@ def tile_axis_aligned_gmm_layer_t_kernel(tc, x, centers, D, out):
                     out=x_sb[:, t0 * DIM : t1 * DIM].rearrange("p (t d) -> p t d", t=t1 - t0), in_=x_v[:, t0:t1, :]
                 )
 
-            load_w(d_v, d_sb, 0)
-            load_w(d_v, d_sb, 1)
+            load_w(d_v, d_sb, 0, 2)
+            load_w(d_v, d_sb, 2, 4)
+            load_w(d_v, d_sb, 4, 8)
             load_x(0, 4)
-            load_w(c_v, c_sb, 0)
-            load_w(c_v, c_sb, 1)
+            load_w(c_v, c_sb, 0, 4)
+            load_w(c_v, c_sb, 4, 8)
             load_x(4, 8)
             for t0 in range(8, NT, 8):
                 load_x(t0, t0 + 8)
             d_i = d_sb[:].bitcast(I32)
             d_w = d_sb[:].bitcast(F32)
             c_w = c_sb[:].bitcast(F32)
-            cg = pro.tile([P, CLS * 4], BF16, name="cg", tag="cg")
-            cg_w = cg[:].bitcast(F32)
             w1g = d_sb
             w2g = c_sb
             lnr = [pro.tile([P, 4 * HC], F32, name="lnr%d" % h, tag="lnr%d" % h) for h in range(2)]
             dv = [pro.tile([P, 4 * HC], F32, name="dv%d" % h, tag="dv%d" % h) for h in range(2)]
+            cdv = [pro.tile([P, 4 * HC], F32, name="cdv%d" % h, tag="cdv%d" % h) for h in range(2)]
             cc = [pro.tile([P, 4 * HC], F32, name="cc", tag="cc")] * 2
             d_t = {}
             c_t = {}
             q_a = {}
 
-            def p_and(h):
-                words = slice(h * 1024, (h + 1) * 1024)
+            def p_and(j0, j1):
+                words = slice(j0 * 256, j1 * 256)
                 nc.vector.tensor_single_scalar(
                     out=d_i[:, words], in_=d_i[:, words], scalar=0x7FFF7FFF, op=ALU.bitwise_and
                 )
@@ -222,10 +213,13 @@ def tile_axis_aligned_gmm_layer_t_kernel(tc, x, centers, D, out):
                         )
 
             def p_rho():
-                nc.vector.tensor_scalar_add(out=a0[:], in0=d_t[(0, 0)][:].bitcast(BF16)[:, 0:1], scalar1=EPS)
+                ref = d_t[(0, 0)][:].bitcast(BF16)[:, 0:1]
+                nc.vector.tensor_scalar_add(out=a0[:, 0:1], in0=ref, scalar1=EPS)
+                nc.vector.tensor_scalar(
+                    out=a0[:, 1:2], in0=ref, scalar1=EPS, scalar2=1.0 / EPS, op0=ALU.add, op1=ALU.mult
+                )
                 nc.vector.reciprocal(out=inv[:], in_=a0[:])
-                nc.vector.tensor_scalar_mul(out=einv[:], in0=inv[:], scalar1=EPS)
-                nc.scalar.activation(out=lninv[:], in_=inv[:], func=ACT.Ln)
+                nc.scalar.activation(out=lninv[:], in_=inv[:, 0:1], func=ACT.Ln)
 
             def p_ln(h, u):
                 nc.scalar.activation(
@@ -233,25 +227,24 @@ def tile_axis_aligned_gmm_layer_t_kernel(tc, x, centers, D, out):
                     in_=d_t[(h, u)][:].bitcast(BF16).rearrange("p (r e) -> p e r", e=2),
                     func=ACT.Ln,
                     scale=inv[:, 0:1],
-                    bias=einv[:, 0:1],
+                    bias=inv[:, 1:2],
                 )
 
             def p_ctr(h, pr):
-                c_t[(h, pr)] = bank("cT", "pc")
+                c_t[(h, pr)] = bank("cT", "pc" if h == 0 else "pd")
                 for jj in range(2):
                     src = (4 * h + 2 * pr + jj) * 256
                     for u in range(2):
-                        dst = (2 * jj + u) * P
+                        dst = (2 * u + jj) * P
                         nc.tensor.transpose(
                             out=c_t[(h, pr)][:, dst : dst + P], in_=c_w[:, src + u : src + 256 : 2], identity=ident[:]
                         )
 
-            def p_cgc(h, pr):
-                w0 = (4 * h + 2 * pr) * P * 2
-                nc.vector.tensor_copy(
-                    out=cg_w[:, w0 : w0 + 512].rearrange("p (j r u) -> p j r u", j=2, u=2),
-                    in_=c_t[(h, pr)][:].rearrange("p (j u r) -> p j r u", j=2, u=2),
-                )
+            def c_tr(h, pc):
+                return c_t[(h, pc)][:].bitcast(BF16).rearrange("p (u r e) -> p u e r", u=2, e=2)
+
+            def f_uer(t, h, pc):
+                return t[h][:].rearrange("p (u e r) -> p u e r", u=2, e=2)[:, :, :, pc * 256 : (pc + 1) * 256]
 
             def f_tr(t, h, pc):
                 return t[h][:].rearrange("p (t r) -> p t r", t=4)[:, :, pc * 256 : (pc + 1) * 256]
@@ -267,30 +260,26 @@ def tile_axis_aligned_gmm_layer_t_kernel(tc, x, centers, D, out):
                     out=f_tr(dv, h, pc), in_=f_tr(lnr, h, pc), func=ACT.Exp, scale=-1.0, bias=lninv[:, 0:1]
                 )
 
-            def p_w1(h, pc, eng):
-                o_ap = w1g[:, g_cols(h, pc)].rearrange("p (r t) -> p r t", t=4)
-                if eng == "V":
-                    nc.vector.tensor_scalar_mul(out=o_ap, in0=f_rt(dv, h, pc), scalar1=0.5)
-                else:
-                    nc.scalar.activation(out=o_ap, in_=f_rt(dv, h, pc), func=ACT.Copy, scale=0.5)
+            def p_w1(h, pc):
+                nc.gpsimd.tensor_scalar(
+                    out=w1g[:, g_cols(h, pc)].rearrange("p (r t) -> p r t", t=4), in0=f_rt(dv, h, pc),
+                    scalar1=0.5, scalar2=0.0, op0=ALU.mult, op1=ALU.add,
+                )
+
+            def p_w2(h, pc):
+                nc.gpsimd.tensor_scalar(
+                    out=w2g[:, g_cols(h, pc)].rearrange("p (r t) -> p r t", t=4), in0=f_rt(cdv, h, pc),
+                    scalar1=-1.0, scalar2=0.0, op0=ALU.mult, op1=ALU.add,
+                )
 
             def p_cd(h, pc):
                 nc.vector.tensor_tensor(
-                    out=f_tr(dv, h, pc), in0=f_tr(dv, h, pc),
-                    in1=cg[:, g_cols(h, pc)].rearrange("p (r t) -> p t r", t=4), op=ALU.mult,
+                    out=f_uer(cdv, h, pc), in0=f_uer(dv, h, pc), in1=c_tr(h, pc), op=ALU.mult
                 )
-
-            def p_w2(h, pc, eng):
-                o_ap = w2g[:, g_cols(h, pc)].rearrange("p (r t) -> p r t", t=4)
-                if eng == "V":
-                    nc.vector.tensor_scalar_mul(out=o_ap, in0=f_rt(dv, h, pc), scalar1=-1.0)
-                else:
-                    nc.scalar.activation(out=o_ap, in_=f_rt(dv, h, pc), func=ACT.Copy, scale=-1.0)
 
             def p_ccd(h, pc):
                 nc.vector.tensor_tensor(
-                    out=f_tr(cc, h, pc), in0=f_tr(dv, h, pc),
-                    in1=cg[:, g_cols(h, pc)].rearrange("p (r t) -> p t r", t=4), op=ALU.mult,
+                    out=f_uer(cc, h, pc), in0=f_uer(cdv, h, pc), in1=c_tr(h, pc), op=ALU.mult
                 )
 
             def p_qw(h, which):
@@ -303,7 +292,7 @@ def tile_axis_aligned_gmm_layer_t_kernel(tc, x, centers, D, out):
 
             def p_at(h, jj):
                 if jj == 0:
-                    q_a[h] = bank("qA", "pa")
+                    q_a[h] = bank("qA", "pc")
                 parts = [(lnr, t) for t in range(4)] + [(cc, t) for t in range(4)]
                 for z in range(8):
                     src, t = parts[z]
@@ -327,7 +316,7 @@ def tile_axis_aligned_gmm_layer_t_kernel(tc, x, centers, D, out):
             b_b = {}
 
             def p_gbt():
-                b_b[0] = bank("bB", "pa")
+                b_b[0] = bank("bB", "pc")
                 for jj in range(4):
                     nc.tensor.transpose(
                         out=b_b[0][:, jj * P : (jj + 1) * P],
@@ -338,93 +327,78 @@ def tile_axis_aligned_gmm_layer_t_kernel(tc, x, centers, D, out):
             def p_gbc():
                 nc.scalar.copy(out=g_b[:], in_=b_b[0][:])
 
-            warm_up(11, ones[:], "pc")
-            p_and(0)
-            p_and(1)
+            p_and(0, 2)
+            p_and(2, 4)
             p_dtr(0)
             p_rho()
-            warm_up(2, ones[:], "pc")
-            x_tr(0, 0)
-            x_cp(0, 0, "V")
+            p_and(4, 8)
             p_dtr(1)
-            warm_up(2, ones[:], "pc")
-            x_tr(0, 1)
-            x_cp(0, 1, "V")
             for h in range(2):
                 for u in range(2):
                     p_ln(h, u)
-            p_ctr(0, 0)
-            p_cgc(0, 0)
-            p_ctr(0, 1)
-            p_cgc(0, 1)
-            warm_up(2, ones[:], "pd")
+            for half in range(2):
+                x_tr(0, half, "pa")
+                x_cp(0, half, "V")
+            for h in range(2):
+                for pr in range(2):
+                    p_ctr(h, pr)
             x_sq(0, 0, 2, "V")
-            for pr in range(2):
-                p_ctr(1, pr)
-                p_cgc(1, pr)
-            warm_up(2, ones[:], "pa")
-            x_tr(1, 0)
-            x_tr(1, 1)
-            warm_up(4, xg[0][:, 2048:2560], "pa")
+            x_tr(1, 0, "pa")
+            x_tr(1, 1, "pa")
             x_qt(0)
             for h in range(2):
                 for pc in range(2):
                     p_exp(h, pc)
             for pc in range(2):
-                p_w1(0, pc, "V")
+                p_w1(0, pc)
                 p_cd(0, pc)
             for pc in range(2):
-                p_w2(0, pc, "V")
+                p_w2(0, pc)
             for pc in range(2):
-                warm_up(4, w1g[:, g_cols(0, pc)][:, 0:512], "pa")
-            p_qw(0, 1)
-            p_qw(0, 2)
-            p_w1(1, 0, "S")
-            p_w1(1, 1, "S")
-            for half in range(2):
-                x_cp(1, half, "S")
-            x_sq(1, 0, 2, "S")
-            warm_up(2, w2g[:, g_cols(0, 1)][:, 0:512], "pa")
-            x_tr(2, 0)
-            x_tr(2, 1)
-            for half in range(2):
-                x_cp(2, half, "S")
-            x_sq(2, 0, 2, "S")
-            for pc in range(2):
-                m_t(0, pc)
                 p_ccd(0, pc)
                 p_at(0, 2 * pc)
                 p_at(0, 2 * pc + 1)
-            warm_up(3, ones[:], "pc")
+            p_qw(0, 1)
+            p_qw(0, 2)
+            for pc in range(2):
+                p_w1(1, pc)
+            for half in range(2):
+                x_cp(1, half, "S")
+            x_sq(1, 0, 2, "S")
             p_cd(1, 0)
-            p_cd(1, 1)
             p_c2(0)
             p_gcol(0)
+            m_t(0, 0)
+            m_t(0, 1)
+            x_tr(2, 0, "pa")
+            x_tr(2, 1, "pa")
             e_v(0, 0)
             e_v(0, 1)
+            p_cd(1, 1)
+            for pc in range(2):
+                p_w2(1, pc)
+            for half in range(2):
+                x_cp(2, half, "S")
             for pc in range(2):
                 m_t(0, 2 + pc)
                 e_v(0, 2 + pc)
                 p_ccd(1, pc)
                 p_at(1, 2 * pc)
                 p_at(1, 2 * pc + 1)
-            warm_up(2, ones[:], "pc")
-            x_tr(3, 0)
-            x_tr(3, 1)
+            x_sq(2, 0, 2, "S")
+            x_tr(3, 0, "pa")
+            x_tr(3, 1, "pa")
             p_qw(1, 1)
+            p_qw(1, 2)
             x_qt(1)
             p_c2(1)
-            p_w2(1, 0, "S")
             p_gcol(1)
-            p_w2(1, 1, "S")
-            warm_up(2, ones[:], "pc")
             p_gbt()
             p_gbc()
-            p_qw(1, 2)
             for half in range(2):
                 x_cp(3, half, "S")
-            x_sq(3, 0, 2, "S")
             x_qt(2)
+            x_sq(3, 0, 2, "S")
 
         o2p = ctx.enter_context(tc.tile_pool(name="o2p", bufs=O2_BUFS))
         o2 = {}
@@ -519,7 +493,7 @@ def tile_axis_aligned_gmm_layer_t_kernel(tc, x, centers, D, out):
             m = n - off
             return (m // 4, m % 4) if 0 <= m < NT else (-1, 0)
 
-        for n in range(MD, NT + SC + 1):
+        for n in range(MD, NT + SC + 2):
             b, i = tile_at(n, BT)
             if b >= 0:
                 b_t(b, i)
@@ -527,7 +501,7 @@ def tile_axis_aligned_gmm_layer_t_kernel(tc, x, centers, D, out):
                     b_t(b, i, 1)
             b, i = tile_at(n, XTR)
             if b >= X_PRO and i % 2 == 0:
-                x_tr(b, i // 2)
+                x_tr(b, i // 2, "pd")
             b, i = tile_at(n, MD)
             if b >= 0 and b not in FULL:
                 m_d(b, i)
@@ -558,7 +532,7 @@ def tile_axis_aligned_gmm_layer_t_kernel(tc, x, centers, D, out):
             b, i = tile_at(n, AD + 1)
             if b >= 0 and i % 2 == 1 and b not in FULL:
                 d_m(b, i // 2)
-            b, i = tile_at(n, 0)
+            b, i = tile_at(n, EX)
             if b >= 0:
                 e_x(b, i)
             b, i = tile_at(n, XCP)

@@ -42,7 +42,7 @@ Q_PRO = 3
 M_PRO = 1
 SQE = "SV"
 LASTV = 1
-SC_COLS = 512
+SC_COLS = 1024
 O2_BUFS = 9
 XG_BUFS = 4
 ST_BUFS = 4

@@ -32,21 +32,23 @@ AD = -4
 BT = -1
 EX = 0
 RC = 1
+RCL = 2
 SC = 3
 XTR = -17
 XCP = -16
 XSQ = -14
 XQ = -9
-X_PRO = 4
+X_PRO = 5
+S_PRO = 4
 Q_PRO = 3
 M_PRO = 1
+SQ3 = "S"
 SQE = "SV"
 LASTV = 1
 SC_COLS = 1024
 O2_BUFS = 9
 XG_BUFS = 4
 ST_BUFS = 4
-FULL = ()
 
 
 def tile_axis_aligned_gmm_layer_t_kernel(tc, x, centers, D, out):
@@ -145,20 +147,20 @@ def tile_axis_aligned_gmm_layer_t_kernel(tc, x, centers, D, out):
                 start=False, stop=True,
             )
 
-        def m_t(b, jj, h=0):
+        def m_t(b, jj):
             if jj == 0:
-                s_t[(b, h)] = stp.tile([P, 4 * 512], F32, name="s_t", tag="s_t")
-            jc = slice(h * HC + jj * P, h * HC + (jj + 1) * P)
-            pt[(b, jj, h)] = bank("pt", "pb")
+                s_t[b] = stp.tile([P, 4 * 512], F32, name="s_t", tag="s_t")
+            jc = slice(jj * P, (jj + 1) * P)
+            pt[(b, jj)] = bank("pt", "pb")
             mx_pair(
-                pt[(b, jj, h)][:], w1c[:, jc], w1s[:, jc], xq[b][:, 512:1024], xs[b][:, 512:1024],
+                pt[(b, jj)][:], w1c[:, jc], w1s[:, jc], xq[b][:, 512:1024], xs[b][:, 512:1024],
                 w2c[:, jc], w2s[:, jc], xq[b][:, 0:512], xs[b][:, 0:512],
             )
 
-        def e_v(b, jj, h=0):
+        def e_v(b, jj):
             nc.scalar.activation(
-                out=s_t[(b, h)][:, jj * 512 : (jj + 1) * 512], in_=pt[(b, jj, h)][:], func=ACT.Identity,
-                bias=gcol[h][:, jj : jj + 1], scale=1.0,
+                out=s_t[b][:, jj * 512 : (jj + 1) * 512], in_=pt[(b, jj)][:], func=ACT.Identity,
+                bias=gcol[0][:, jj : jj + 1], scale=1.0,
             )
 
         with tc.tile_pool(name="pro", bufs=1) as pro:
@@ -349,6 +351,13 @@ def tile_axis_aligned_gmm_layer_t_kernel(tc, x, centers, D, out):
             for h in range(2):
                 for pc in range(2):
                     p_exp(h, pc)
+            for half in range(2):
+                x_cp(1, half, "S")
+            x_tr(2, 0, "pa")
+            x_tr(2, 1, "pa")
+            x_sq(1, 0, 2, "S")
+            for half in range(2):
+                x_cp(2, half, "S")
             for pc in range(2):
                 p_w1(0, pc)
                 p_cd(0, pc)
@@ -362,32 +371,29 @@ def tile_axis_aligned_gmm_layer_t_kernel(tc, x, centers, D, out):
             p_qw(0, 2)
             for pc in range(2):
                 p_w1(1, pc)
-            for half in range(2):
-                x_cp(1, half, "S")
-            x_sq(1, 0, 2, "S")
             p_cd(1, 0)
             p_c2(0)
             p_gcol(0)
             m_t(0, 0)
             m_t(0, 1)
-            x_tr(2, 0, "pa")
-            x_tr(2, 1, "pa")
+            x_tr(3, 0, "pa")
+            x_tr(3, 1, "pa")
             e_v(0, 0)
             e_v(0, 1)
+            x_sq(2, 0, 2, "S")
             p_cd(1, 1)
             for pc in range(2):
                 p_w2(1, pc)
-            for half in range(2):
-                x_cp(2, half, "S")
             for pc in range(2):
                 m_t(0, 2 + pc)
                 e_v(0, 2 + pc)
                 p_ccd(1, pc)
                 p_at(1, 2 * pc)
                 p_at(1, 2 * pc + 1)
-            x_sq(2, 0, 2, "S")
-            x_tr(3, 0, "pa")
-            x_tr(3, 1, "pa")
+            for half in range(2):
+                x_cp(3, half, "S")
+            x_tr(4, 0, "pa")
+            x_tr(4, 1, "pa")
             p_qw(1, 1)
             p_qw(1, 2)
             x_qt(1)
@@ -395,16 +401,15 @@ def tile_axis_aligned_gmm_layer_t_kernel(tc, x, centers, D, out):
             p_gcol(1)
             p_gbt()
             p_gbc()
-            for half in range(2):
-                x_cp(3, half, "S")
-            x_qt(2)
             x_sq(3, 0, 2, "S")
+            x_qt(2)
+            for half in range(2):
+                x_cp(4, half, "S")
 
         o2p = ctx.enter_context(tc.tile_pool(name="o2p", bufs=O2_BUFS))
         o2 = {}
         dmin = {}
         nmin = {}
-        nmin0 = {}
         sums = {}
         rec = {}
 
@@ -437,22 +442,19 @@ def tile_axis_aligned_gmm_layer_t_kernel(tc, x, centers, D, out):
                 axis=AX.X, op=ALU.min,
             )
 
-        def b_t(b, i, h=0):
-            st[(b, i, h)] = bank("st", "pa" if h == 0 else "pc")
+        def b_t(b, i):
+            st[(b, i)] = bank("st", "pa")
             for jj in range(4):
                 nc.tensor.transpose(
-                    out=st[(b, i, h)][:, jj * P : (jj + 1) * P],
-                    in_=s_t[(b, h)][:, jj * 512 + i * P : jj * 512 + (i + 1) * P],
+                    out=st[(b, i)][:, jj * P : (jj + 1) * P],
+                    in_=s_t[b][:, jj * 512 + i * P : jj * 512 + (i + 1) * P],
                     identity=ident[:],
                 )
 
-        def e_m(b, i, h=0):
-            prev = dmin if h == 0 else nmin0
-            now = nmin0 if (h == 0 and b in FULL) else nmin
+        def e_m(b, i):
             nc.vector.tensor_scalar(
-                out=o_cols(b, i, h * HC, (h + 1) * HC), in0=st[(b, i, h)][:], scalar1=0.0,
-                scalar2=None if (h == 0 and b in FULL) else col(prev, b, i),
-                op0=ALU.add, op1=ALU.min, accum_out=col(now, b, i),
+                out=o_cols(b, i, 0, HC), in0=st[(b, i)][:], scalar1=0.0, scalar2=col(dmin, b, i),
+                op0=ALU.add, op1=ALU.min, accum_out=col(nmin, b, i),
             )
 
         def e_x(b, i):
@@ -493,44 +495,30 @@ def tile_axis_aligned_gmm_layer_t_kernel(tc, x, centers, D, out):
             m = n - off
             return (m // 4, m % 4) if 0 <= m < NT else (-1, 0)
 
-        for n in range(MD, NT + SC + 2):
+        for n in range(MD, NT + SC + 3):
             b, i = tile_at(n, BT)
             if b >= 0:
                 b_t(b, i)
-                if b in FULL:
-                    b_t(b, i, 1)
             b, i = tile_at(n, XTR)
             if b >= X_PRO and i % 2 == 0:
                 x_tr(b, i // 2, "pd")
             b, i = tile_at(n, MD)
-            if b >= 0 and b not in FULL:
+            if b >= 0:
                 m_d(b, i)
             b, i = tile_at(n, MT)
             if b >= M_PRO:
                 m_t(b, i)
-                if b in FULL:
-                    m_t(b, i, 1)
             b, i = tile_at(n, 0)
             if b >= 0:
-                if b in FULL:
-                    if i % 2 == 0:
-                        o2[(b, i // 2)] = o2p.tile([P, 2 * CLS], F32, name="o2", tag="o2")
-                        nmin0[(b, i // 2)] = small.tile([P, 2], F32, name="nmin0", tag="nmin0")
-                        nmin[(b, i // 2)] = small.tile([P, 2], F32, name="nmin", tag="nmin")
-                    e_m(b, i)
-                    e_m(b, i, 1)
-                else:
-                    e_m(b, i)
+                e_m(b, i)
             b, i = tile_at(n, EV)
             if b >= M_PRO:
                 e_v(b, i)
-                if b in FULL:
-                    e_v(b, i, 1)
             b, i = tile_at(n, AD)
-            if b >= 0 and b not in FULL:
+            if b >= 0:
                 a_d(b, i)
             b, i = tile_at(n, AD + 1)
-            if b >= 0 and i % 2 == 1 and b not in FULL:
+            if b >= 0 and i % 2 == 1:
                 d_m(b, i // 2)
             b, i = tile_at(n, EX)
             if b >= 0:
@@ -539,17 +527,18 @@ def tile_axis_aligned_gmm_layer_t_kernel(tc, x, centers, D, out):
             if b >= X_PRO and i % 2 == 0:
                 x_cp(b, i // 2, "S")
             b, i = tile_at(n, XSQ)
-            if b >= X_PRO and i % 2 == 0:
+            if b >= S_PRO and i % 2 == 0:
                 x_sq(b, i // 2, 1, SQE[(2 * b + i // 2) % len(SQE)])
             b, i = tile_at(n, XQ)
             if b >= Q_PRO and i == 0:
                 x_qt(b)
-            b, i = tile_at(n, RC)
+            b, i = tile_at(n, RCL)
             if b >= NB - LASTV:
                 r_c1(b, i)
                 s_c(b, i, "V")
                 store1(b, i)
-            elif b >= 0 and i % 2 == 1:
+            b, i = tile_at(n, RC)
+            if 0 <= b < NB - LASTV and i % 2 == 1:
                 r_c(b, i // 2)
             b, i = tile_at(n, SC)
             if 0 <= b < NB - LASTV:

@@ -37,7 +37,7 @@ SC = 3
 XTR = -17
 XCP = -16
 XSQ = -14
-XQ = -9
+XQ = -10
 X_PRO = 5
 S_PRO = 4
 Q_PRO = 3

from contextlib import ExitStack

import concourse.mybir as mybir
from concourse.masks import make_identity

F32 = mybir.dt.float32
BF16 = mybir.dt.bfloat16
I32 = mybir.dt.int32
U32 = mybir.dt.uint32
U8 = mybir.dt.uint8
FP8X4 = mybir.dt.float8_e4m3fn_x4
ALU = mybir.AluOpType
ACT = mybir.ActivationFunctionType
AX = mybir.AxisListType

P = 128
ROWS = 5120
CLS = 1024
DIM = 512
NT = ROWS // P
NB = NT // 4
CT = CLS // P
HC = CLS // 2
EPS = 1e-4

FLOPS = 2 * 2 * ROWS * CLS * DIM

MT = -6
EV = -5
MD = -5
AD = -4
BT = -1
EX = 0
RC = 1
RCL = 2
SC = 3
XTR = -17
XCP = -16
XSQ = -14
XQ = -10
X_PRO = 5
S_PRO = 4
Q_PRO = 3
M_PRO = 1
SQ3 = "S"
SQE = "SV"
LASTV = 1
SC_COLS = 1024
O2_BUFS = 9
XG_BUFS = 4
ST_BUFS = 4


def tile_axis_aligned_gmm_layer_t_kernel(tc, x, centers, D, out):
    nc = tc.nc
    with ExitStack() as ctx:
        ctx.enter_context(tc.manual_schedule())
        const = ctx.enter_context(tc.tile_pool(name="const", bufs=1))
        small = ctx.enter_context(tc.tile_pool(name="small", bufs=8))
        xgp = ctx.enter_context(tc.tile_pool(name="xgp", bufs=XG_BUFS))
        xqp = ctx.enter_context(tc.tile_pool(name="xqp", bufs=6))
        stp = ctx.enter_context(tc.tile_pool(name="stp", bufs=ST_BUFS))
        ps = ctx.enter_context(tc.psum_pool(name="ps", bufs=2))

        def bank(nm, tag):
            return ps.tile([P, 512], F32, name=nm, tag=tag)

        one = const.tile([P, 1], F32, name="one", tag="one")
        nc.vector.memset(one[:], 1.0)
        warm = const.tile([P, 1], F32, name="warm", tag="warm")
        nc.scalar.activation(out=warm[:], in_=one[:], func=ACT.Ln)
        ident = const.tile([P, P], F32, name="ident", tag="ident")
        make_identity(nc, ident[:])

        x_sb = const.tile([P, NT * DIM], BF16, name="x_sb", tag="x_sb")
        w1c = const.tile([P, CLS], U32, name="w1c", tag="w1c", align_bytes=64)
        w2c = const.tile([P, CLS], U32, name="w2c", tag="w2c", align_bytes=64)
        w1s = const.tile([P, CLS], U8, name="w1s", tag="w1s", align_bytes=64)
        w2s = const.tile([P, CLS], U8, name="w2s", tag="w2s", align_bytes=64)
        g_b = const.tile([P, HC], F32, name="g_b", tag="g_b")
        gcol = [const.tile([P, 4], F32, name="gcol%d" % h, tag="gcol%d" % h) for h in range(2)]
        c2col = [const.tile([P, 4], F32, name="c2col%d" % h, tag="c2col%d" % h) for h in range(2)]
        a0 = const.tile([P, 2], F32, name="a0", tag="a0")
        inv = const.tile([P, 2], F32, name="inv", tag="inv")
        lninv = const.tile([P, 1], F32, name="lninv", tag="lninv")
        x_w = x_sb[:].bitcast(F32)
        x_v = x.rearrange("(p t) d -> p t d", t=NT)
        out_v = out.rearrange("(p t) k -> p t k", t=NT)
        d_v = D.rearrange("(j p) d -> p j d", p=P)
        c_v = centers.rearrange("(j p) d -> p j d", p=P)

        xg = {}
        xt = {}
        xq = {}
        xs = {}
        s_t = {}
        pt = {}
        acc = {}
        st = {}

        def x_tr(b, half, tag):
            xt[(b, half)] = bank("xT", tag)
            for i in range(2):
                src = (4 * b + 2 * half + i) * 256
                for u in range(2):
                    dst = (2 * i + u) * P
                    nc.tensor.transpose(
                        out=xt[(b, half)][:, dst : dst + P], in_=x_w[:, src + u : src + 256 : 2], identity=ident[:]
                    )

        def x_cp(b, half, eng):
            if half == 0:
                xg[b] = xgp.tile([P, 2 * 2048], BF16, name="xg", tag="xg", align_bytes=64)
            o_ap = xg[b][:].bitcast(F32)[:, half * 512 : (half + 1) * 512].rearrange("p (i r u) -> p i r u", i=2, u=2)
            i_ap = xt[(b, half)][:].rearrange("p (i u r) -> p i r u", i=2, u=2)
            if eng == "V":
                nc.vector.tensor_copy(out=o_ap, in_=i_ap)
            else:
                nc.scalar.copy(out=o_ap, in_=i_ap)

        def x_sq(b, z, n, eng):
            zi = slice(z * 1024, (z + n) * 1024)
            zo = slice(2048 + z * 1024, 2048 + (z + n) * 1024)
            if eng == "S":
                nc.scalar.activation(out=xg[b][:, zo], in_=xg[b][:, zi], func=ACT.Square)
            elif eng == "V":
                nc.vector.tensor_tensor(out=xg[b][:, zo], in0=xg[b][:, zi], in1=xg[b][:, zi], op=ALU.mult)
            else:
                for c in range(z * 1024, (z + n) * 1024, 512):
                    nc.gpsimd.tensor_tensor(
                        out=xg[b][:, 2048 + c : 2048 + c + 512], in0=xg[b][:, c : c + 512], in1=xg[b][:, c : c + 512],
                        op=ALU.mult,
                    )

        def x_qt(b):
            xq[b] = xqp.tile([P, 1024], U32, name="xq", tag="xq", align_bytes=64)
            xs[b] = xqp.tile([P, 1024], U8, name="xs", tag="xs", align_bytes=64)
            nc.vector.quantize_mx(out=xq[b][:].bitcast(FP8X4), scales=xs[b][:], in_=xg[b][:])

        def mx_pair(dst, l1, l1s, r1, r1s, l2, l2s, r2, r2s):
            nc.tensor.matmul_mx(
                out=dst, lhsT=l1.bitcast(FP8X4), lhsT_scale=l1s, rhs=r1.bitcast(FP8X4), rhs_scale=r1s,
                start=True, stop=False,
            )
            nc.tensor.matmul_mx(
                out=dst, lhsT=l2.bitcast(FP8X4), lhsT_scale=l2s, rhs=r2.bitcast(FP8X4), rhs_scale=r2s,
                start=False, stop=True,
            )

        def m_t(b, jj):
            if jj == 0:
                s_t[b] = stp.tile([P, 4 * 512], F32, name="s_t", tag="s_t")
            jc = slice(jj * P, (jj + 1) * P)
            pt[(b, jj)] = bank("pt", "pb")
            mx_pair(
                pt[(b, jj)][:], w1c[:, jc], w1s[:, jc], xq[b][:, 512:1024], xs[b][:, 512:1024],
                w2c[:, jc], w2s[:, jc], xq[b][:, 0:512], xs[b][:, 0:512],
            )

        def e_v(b, jj):
            nc.scalar.activation(
                out=s_t[b][:, jj * 512 : (jj + 1) * 512], in_=pt[(b, jj)][:], func=ACT.Identity,
                bias=gcol[0][:, jj : jj + 1], scale=1.0,
            )

        with tc.tile_pool(name="pro", bufs=1) as pro:
            d_sb = pro.tile([P, CT * DIM], BF16, name="d_sb", tag="d_sb", align_bytes=64)
            c_sb = pro.tile([P, CT * DIM], BF16, name="c_sb", tag="c_sb", align_bytes=64)

            def load_w(src_v, dst_t, j0, j1):
                nc.sync.dma_start(
                    out=dst_t[:, j0 * DIM : j1 * DIM].rearrange("p (j d) -> p j d", j=j1 - j0), in_=src_v[:, j0:j1, :]
                )

            def load_x(t0, t1):
                nc.sync.dma_start(
                    out=x_sb[:, t0 * DIM : t1 * DIM].rearrange("p (t d) -> p t d", t=t1 - t0), in_=x_v[:, t0:t1, :]
                )

            load_w(d_v, d_sb, 0, 2)
            load_w(d_v, d_sb, 2, 4)
            load_w(d_v, d_sb, 4, 8)
            load_x(0, 4)
            load_w(c_v, c_sb, 0, 4)
            load_w(c_v, c_sb, 4, 8)
            load_x(4, 8)
            for t0 in range(8, NT, 8):
                load_x(t0, t0 + 8)
            d_i = d_sb[:].bitcast(I32)
            d_w = d_sb[:].bitcast(F32)
            c_w = c_sb[:].bitcast(F32)
            w1g = d_sb
            w2g = c_sb
            lnr = [pro.tile([P, 4 * HC], F32, name="lnr%d" % h, tag="lnr%d" % h) for h in range(2)]
            dv = [pro.tile([P, 4 * HC], F32, name="dv%d" % h, tag="dv%d" % h) for h in range(2)]
            cdv = [pro.tile([P, 4 * HC], F32, name="cdv%d" % h, tag="cdv%d" % h) for h in range(2)]
            cc = [pro.tile([P, 4 * HC], F32, name="cc", tag="cc")] * 2
            d_t = {}
            c_t = {}
            q_a = {}

            def p_and(j0, j1):
                words = slice(j0 * 256, j1 * 256)
                nc.vector.tensor_single_scalar(
                    out=d_i[:, words], in_=d_i[:, words], scalar=0x7FFF7FFF, op=ALU.bitwise_and
                )

            def p_dtr(h):
                for u in range(2):
                    d_t[(h, u)] = bank("dT", "pa" if h == 0 else "pb")
                    for jj in range(4):
                        src = (4 * h + jj) * 256
                        nc.tensor.transpose(
                            out=d_t[(h, u)][:, jj * P : (jj + 1) * P], in_=d_w[:, src + u : src + 256 : 2], identity=ident[:]
                        )

            def p_rho():
                ref = d_t[(0, 0)][:].bitcast(BF16)[:, 0:1]
                nc.vector.tensor_scalar_add(out=a0[:, 0:1], in0=ref, scalar1=EPS)
                nc.vector.tensor_scalar(
                    out=a0[:, 1:2], in0=ref, scalar1=EPS, scalar2=1.0 / EPS, op0=ALU.add, op1=ALU.mult
                )
                nc.vector.reciprocal(out=inv[:], in_=a0[:])
                nc.scalar.activation(out=lninv[:], in_=inv[:, 0:1], func=ACT.Ln)

            def p_ln(h, u):
                nc.scalar.activation(
                    out=lnr[h][:, 2 * u * HC : (2 * u + 2) * HC].rearrange("p (e r) -> p e r", e=2),
                    in_=d_t[(h, u)][:].bitcast(BF16).rearrange("p (r e) -> p e r", e=2),
                    func=ACT.Ln,
                    scale=inv[:, 0:1],
                    bias=inv[:, 1:2],
                )

            def p_ctr(h, pr):
                c_t[(h, pr)] = bank("cT", "pc" if h == 0 else "pd")
                for jj in range(2):
                    src = (4 * h + 2 * pr + jj) * 256
                    for u in range(2):
                        dst = (2 * u + jj) * P
                        nc.tensor.transpose(
                            out=c_t[(h, pr)][:, dst : dst + P], in_=c_w[:, src + u : src + 256 : 2], identity=ident[:]
                        )

            def c_tr(h, pc):
                return c_t[(h, pc)][:].bitcast(BF16).rearrange("p (u r e) -> p u e r", u=2, e=2)

            def f_uer(t, h, pc):
                return t[h][:].rearrange("p (u e r) -> p u e r", u=2, e=2)[:, :, :, pc * 256 : (pc + 1) * 256]

            def f_tr(t, h, pc):
                return t[h][:].rearrange("p (t r) -> p t r", t=4)[:, :, pc * 256 : (pc + 1) * 256]

            def f_rt(t, h, pc):
                return t[h][:].rearrange("p (t r) -> p r t", t=4)[:, pc * 256 : (pc + 1) * 256, :]

            def g_cols(h, pc):
                return slice((h * HC + pc * 256) * 4, (h * HC + (pc + 1) * 256) * 4)

            def p_exp(h, pc):
                nc.scalar.activation(
                    out=f_tr(dv, h, pc), in_=f_tr(lnr, h, pc), func=ACT.Exp, scale=-1.0, bias=lninv[:, 0:1]
                )

            def p_w1(h, pc):
                nc.gpsimd.tensor_scalar(
                    out=w1g[:, g_cols(h, pc)].rearrange("p (r t) -> p r t", t=4), in0=f_rt(dv, h, pc),
                    scalar1=0.5, scalar2=0.0, op0=ALU.mult, op1=ALU.add,
                )

            def p_w2(h, pc):
                nc.gpsimd.tensor_scalar(
                    out=w2g[:, g_cols(h, pc)].rearrange("p (r t) -> p r t", t=4), in0=f_rt(cdv, h, pc),
                    scalar1=-1.0, scalar2=0.0, op0=ALU.mult, op1=ALU.add,
                )

            def p_cd(h, pc):
                nc.vector.tensor_tensor(
                    out=f_uer(cdv, h, pc), in0=f_uer(dv, h, pc), in1=c_tr(h, pc), op=ALU.mult
                )

            def p_ccd(h, pc):
                nc.vector.tensor_tensor(
                    out=f_uer(cc, h, pc), in0=f_uer(cdv, h, pc), in1=c_tr(h, pc), op=ALU.mult
                )

            def p_qw(h, which):
                hc = slice(h * HC, (h + 1) * HC)
                hg = slice(h * HC * 4, (h + 1) * HC * 4)
                if which == 1:
                    nc.vector.quantize_mx(out=w1c[:, hc].bitcast(FP8X4), scales=w1s[:, hc], in_=w1g[:, hg])
                else:
                    nc.vector.quantize_mx(out=w2c[:, hc].bitcast(FP8X4), scales=w2s[:, hc], in_=w2g[:, hg])

            def p_at(h, jj):
                if jj == 0:
                    q_a[h] = bank("qA", "pc")
                parts = [(lnr, t) for t in range(4)] + [(cc, t) for t in range(4)]
                for z in range(8):
                    src, t = parts[z]
                    nc.tensor.matmul(
                        out=q_a[h][:, jj * P : (jj + 1) * P],
                        lhsT=src[h][:, t * HC + jj * P : t * HC + (jj + 1) * P],
                        rhs=ident[:],
                        is_transpose=True,
                        start=(z == 0),
                        stop=(z == 7),
                    )

            def p_c2(h):
                nc.vector.tensor_reduce(
                    out=c2col[h][:], in_=q_a[h][:].rearrange("p (j r) -> p j r", j=4), axis=AX.X, op=ALU.add
                )

            def p_gcol(h):
                nc.scalar.mul(gcol[h][:], c2col[h][:], 0.5)

            b_b = {}

            def p_gbt():
                b_b[0] = bank("bB", "pc")
                for jj in range(4):
                    nc.tensor.transpose(
                        out=b_b[0][:, jj * P : (jj + 1) * P],
                        in_=gcol[1][:, jj : jj + 1].to_broadcast([P, P]),
                        identity=ident[:],
                    )

            def p_gbc():
                nc.scalar.copy(out=g_b[:], in_=b_b[0][:])

            p_and(0, 2)
            p_and(2, 4)
            p_dtr(0)
            p_rho()
            p_and(4, 8)
            p_dtr(1)
            for h in range(2):
                for u in range(2):
                    p_ln(h, u)
            for half in range(2):
                x_tr(0, half, "pa")
                x_cp(0, half, "V")
            for h in range(2):
                for pr in range(2):
                    p_ctr(h, pr)
            x_sq(0, 0, 2, "V")
            x_tr(1, 0, "pa")
            x_tr(1, 1, "pa")
            x_qt(0)
            for h in range(2):
                for pc in range(2):
                    p_exp(h, pc)
            for half in range(2):
                x_cp(1, half, "S")
            x_tr(2, 0, "pa")
            x_tr(2, 1, "pa")
            x_sq(1, 0, 2, "S")
            for half in range(2):
                x_cp(2, half, "S")
            for pc in range(2):
                p_w1(0, pc)
                p_cd(0, pc)
            for pc in range(2):
                p_w2(0, pc)
            for pc in range(2):
                p_ccd(0, pc)
                p_at(0, 2 * pc)
                p_at(0, 2 * pc + 1)
            p_qw(0, 1)
            p_qw(0, 2)
            for pc in range(2):
                p_w1(1, pc)
            p_cd(1, 0)
            p_c2(0)
            p_gcol(0)
            m_t(0, 0)
            m_t(0, 1)
            x_tr(3, 0, "pa")
            x_tr(3, 1, "pa")
            e_v(0, 0)
            e_v(0, 1)
            x_sq(2, 0, 2, "S")
            p_cd(1, 1)
            for pc in range(2):
                p_w2(1, pc)
            for pc in range(2):
                m_t(0, 2 + pc)
                e_v(0, 2 + pc)
                p_ccd(1, pc)
                p_at(1, 2 * pc)
                p_at(1, 2 * pc + 1)
            for half in range(2):
                x_cp(3, half, "S")
            x_tr(4, 0, "pa")
            x_tr(4, 1, "pa")
            p_qw(1, 1)
            p_qw(1, 2)
            x_qt(1)
            p_c2(1)
            p_gcol(1)
            p_gbt()
            p_gbc()
            x_sq(3, 0, 2, "S")
            x_qt(2)
            for half in range(2):
                x_cp(4, half, "S")

        o2p = ctx.enter_context(tc.tile_pool(name="o2p", bufs=O2_BUFS))
        o2 = {}
        dmin = {}
        nmin = {}
        sums = {}
        rec = {}

        def o_cols(b, i, c0, c1):
            return o2[(b, i // 2)][:, (i % 2) * CLS + c0 : (i % 2) * CLS + c1]

        def col(t, b, i):
            return t[(b, i // 2)][:, i % 2 : i % 2 + 1]

        def m_d(b, i):
            rc = slice(i * P, (i + 1) * P)
            rc2 = slice(512 + i * P, 512 + (i + 1) * P)
            hc = slice(HC, CLS)
            acc[(b, i)] = bank("acc", "pc")
            mx_pair(
                acc[(b, i)][:], xq[b][:, rc2], xs[b][:, rc2], w1c[:, hc], w1s[:, hc],
                xq[b][:, rc], xs[b][:, rc], w2c[:, hc], w2s[:, hc],
            )

        def a_d(b, i):
            if i % 2 == 0:
                o2[(b, i // 2)] = o2p.tile([P, 2 * CLS], F32, name="o2", tag="o2")
            nc.vector.tensor_tensor(out=o_cols(b, i, HC, CLS), in0=acc[(b, i)][:], in1=g_b[:], op=ALU.add)

        def d_m(b, pr):
            dmin[(b, pr)] = small.tile([P, 2], F32, name="dmin", tag="dmin")
            nmin[(b, pr)] = small.tile([P, 2], F32, name="nmin", tag="nmin")
            nc.vector.tensor_reduce(
                out=dmin[(b, pr)][:], in_=o2[(b, pr)][:].rearrange("p (i k) -> p i k", i=2)[:, :, HC:CLS],
                axis=AX.X, op=ALU.min,
            )

        def b_t(b, i):
            st[(b, i)] = bank("st", "pa")
            for jj in range(4):
                nc.tensor.transpose(
                    out=st[(b, i)][:, jj * P : (jj + 1) * P],
                    in_=s_t[b][:, jj * 512 + i * P : jj * 512 + (i + 1) * P],
                    identity=ident[:],
                )

        def e_m(b, i):
            nc.vector.tensor_scalar(
                out=o_cols(b, i, 0, HC), in0=st[(b, i)][:], scalar1=0.0, scalar2=col(dmin, b, i),
                op0=ALU.add, op1=ALU.min, accum_out=col(nmin, b, i),
            )

        def e_x(b, i):
            if i % 2 == 0:
                sums[(b, i // 2)] = small.tile([P, 2], F32, name="sums", tag="sums")
                rec[(b, i // 2)] = small.tile([P, 2], F32, name="rec", tag="rec")
            nc.scalar.activation(
                out=o_cols(b, i, 0, CLS), in_=o_cols(b, i, 0, CLS), func=ACT.Exp, bias=col(nmin, b, i), scale=-1.0,
                accum_out=col(sums, b, i),
            )

        def r_c(b, pr):
            nc.vector.reciprocal(out=rec[(b, pr)][:], in_=sums[(b, pr)][:])

        def r_c1(b, i):
            nc.vector.reciprocal(out=col(rec, b, i), in_=col(sums, b, i))

        def s_c(b, i, eng="G"):
            if eng == "V":
                nc.vector.tensor_scalar_mul(out=o_cols(b, i, 0, CLS), in0=o_cols(b, i, 0, CLS), scalar1=col(rec, b, i))
                return
            for c0 in range(0, CLS, SC_COLS):
                ap = o_cols(b, i, c0, c0 + SC_COLS)
                nc.gpsimd.tensor_scalar(
                    out=ap, in0=ap, scalar1=col(rec, b, i), scalar2=0.0, op0=ALU.mult, op1=ALU.add
                )

        def store1(b, i):
            nc.sync.dma_start(out=out_v[:, 4 * b + i, :], in_=o_cols(b, i, 0, CLS))

        def store2(b, pr):
            t0 = 4 * b + 2 * pr
            nc.sync.dma_start(
                out=out_v[:, t0 : t0 + 2, :], in_=o2[(b, pr)][:].rearrange("p (i k) -> p i k", i=2)
            )

        def tile_at(n, off):
            m = n - off
            return (m // 4, m % 4) if 0 <= m < NT else (-1, 0)

        for n in range(MD, NT + SC + 3):
            b, i = tile_at(n, BT)
            if b >= 0:
                b_t(b, i)
            b, i = tile_at(n, XTR)
            if b >= X_PRO and i % 2 == 0:
                x_tr(b, i // 2, "pd")
            b, i = tile_at(n, MD)
            if b >= 0:
                m_d(b, i)
            b, i = tile_at(n, MT)
            if b >= M_PRO:
                m_t(b, i)
            b, i = tile_at(n, 0)
            if b >= 0:
                e_m(b, i)
            b, i = tile_at(n, EV)
            if b >= M_PRO:
                e_v(b, i)
            b, i = tile_at(n, AD)
            if b >= 0:
                a_d(b, i)
            b, i = tile_at(n, AD + 1)
            if b >= 0 and i % 2 == 1:
                d_m(b, i // 2)
            b, i = tile_at(n, EX)
            if b >= 0:
                e_x(b, i)
            b, i = tile_at(n, XCP)
            if b >= X_PRO and i % 2 == 0:
                x_cp(b, i // 2, "S")
            b, i = tile_at(n, XSQ)
            if b >= S_PRO and i % 2 == 0:
                x_sq(b, i // 2, 1, SQE[(2 * b + i // 2) % len(SQE)])
            b, i = tile_at(n, XQ)
            if b >= Q_PRO and i == 0:
                x_qt(b)
            b, i = tile_at(n, RCL)
            if b >= NB - LASTV:
                r_c1(b, i)
                s_c(b, i, "V")
                store1(b, i)
            b, i = tile_at(n, RC)
            if 0 <= b < NB - LASTV and i % 2 == 1:
                r_c(b, i // 2)
            b, i = tile_at(n, SC)
            if 0 <= b < NB - LASTV:
                s_c(b, i)
                if b >= NB - LASTV - 1:
                    store1(b, i)
                elif i % 2 == 1:
                    store2(b, i // 2)
